import numpy as np
import ml_dtypes


def mxq(x, axis, fmt="e4m3"):
    dtype, down = {"e4m3": (ml_dtypes.float8_e4m3fn, 7), "e5m2": (ml_dtypes.float8_e5m2, 14)}[fmt]
    v = np.moveaxis(np.asarray(x, np.float32).astype(ml_dtypes.bfloat16).astype(np.float64), axis, -1)
    blocks = v.reshape(v.shape[:-1] + (-1, 32))
    amax = np.abs(blocks).max(-1, keepdims=True)
    byte = np.maximum(np.where(amax > 0, np.frexp(amax)[1] - 1 + 127, 0) - down, 1)
    scale = np.exp2(byte - 127.0)
    codes = (blocks / scale).astype(np.float32).astype(dtype).astype(np.float64)
    return np.moveaxis((codes * scale).reshape(v.shape), -1, axis)


WIDE = False


def mx_kscale(k):
    if not WIDE:
        return np.ones(k)
    levels = np.array([10, -10, 5, -5, 0])
    a = np.random.permutation(np.resize(levels, k // 512 * 4)).reshape(k // 512, 4)
    idx = np.arange(k)
    return np.exp2(a[idx // 512, idx % 128 // 32])


BF16 = ml_dtypes.bfloat16


def bf(x):
    return np.asarray(x, np.float32).astype(BF16)


def f64(x):
    return np.asarray(x).astype(np.float64)


E2M1 = np.array([0.0, 0.5, 1.0, 1.5, 2.0, 3.0, 4.0, 6.0, -0.0, -0.5, -1.0, -1.5, -2.0, -3.0, -4.0, -6.0])


def pack_weight(w, fmt):
    k, n = w.shape
    w = f64(bf(w)).reshape(k // 32, 32, n)
    amax = np.abs(w).max(1)
    if fmt == "e4m3":
        byte = np.frexp(amax)[1] - 1 + 127 - 7
    else:
        mant, ex = np.frexp(amax / 6.0)
        byte = np.where(mant > 0.5, ex, ex - 1) + 127
    byte = np.clip(np.where(amax > 0, byte, 1), 1, 254)
    scaled = (w * np.exp2(127.0 - byte)[:, None, :]).reshape(k, n).astype(np.float32)
    by_word = np.ascontiguousarray(scaled.reshape(k // 512, 128, 4, n).transpose(0, 1, 3, 2))
    if fmt == "e4m3":
        words = by_word.astype(ml_dtypes.float8_e4m3fn).view(np.uint8)
    else:
        c = by_word.astype(ml_dtypes.float4_e2m1fn).view(np.uint8) & 0xF
        words = c[..., 0::2] | (c[..., 1::2] << 4)
    return np.ascontiguousarray(words), np.ascontiguousarray(byte.astype(np.uint8).reshape(k // 512, 16, n))


def unpack_weight(words, scales, fmt):
    g, p, n, _ = words.shape
    if fmt == "e4m3":
        vals = np.ascontiguousarray(words).view(ml_dtypes.float8_e4m3fn).astype(np.float64)
    else:
        nib = np.empty((g, p, n, 4), np.uint8)
        nib[..., 0::2] = words & 0xF
        nib[..., 1::2] = words >> 4
        vals = E2M1[nib]
    vals = vals * np.repeat(np.exp2(scales.astype(np.float64) - 127.0), 8, axis=1)[..., None]
    return vals.transpose(0, 1, 3, 2).reshape(g * 512, n)


B, C, K, BK, BN = 1024, 2048, 2048, 1, 16
KEEP = 0.3
FMT = "e4m3"


def setup_inputs():
    s = mx_kscale(C)
    x = np.random.standard_normal((B, C)) * s
    weight = np.random.uniform(-1.0, 1.0, (K, C)) * 3.2 / np.sqrt(C)
    blk = (np.random.uniform(0.0, 1.0, (K // BK, C // BN)) < KEEP).astype(np.float64)
    mask = np.repeat(np.repeat(blk, BK, axis=0), BN, axis=1)
    weight = weight * mask / s[None, :]
    bias = np.random.uniform(-1.0, 1.0, K) * 0.5
    words, scales = pack_weight(np.ascontiguousarray(weight.T), FMT)
    return {"x": bf(x), "weight_words": words, "weight_scales": scales, "bias": bf(bias)}


def reference(x, weight_words, weight_scales, bias):
    return np.maximum((mxq(f64(x), 1, "e4m3") @ unpack_weight(weight_words, weight_scales, FMT)) + f64(bias), 0.0)

@@ -1,0 +1,156 @@
+from contextlib import ExitStack
+
+import concourse.mybir as mybir
+from concourse.masks import make_identity
+
+F32 = mybir.dt.float32
+BF16 = mybir.dt.bfloat16
+I32 = mybir.dt.int32
+U32 = mybir.dt.uint32
+U8 = mybir.dt.uint8
+FP8X4 = mybir.dt.float8_e4m3fn_x4
+
+P = 128
+PACK = 4
+K_PASS = P * PACK
+PAIRS = PACK // 2
+
+ROWS = 1024
+K = 2048
+N = 2048
+N_CHUNK = 512
+
+ROW_TILES = ROWS // P
+PASSES = K // K_PASS
+CHUNKS = N // N_CHUNK
+WORDS_PER_PASS = K_PASS // 2
+PLANE_ROWS = 4
+QUADRANTS = 4
+
+FLOPS = 2 * ROWS * K * N
+
+
+def tile_sparselinearrelu_kernel(tc, x, weight_words, weight_scales, bias, out):
+    nc = tc.nc
+    with ExitStack() as ctx:
+        ctx.enter_context(tc.manual_schedule())
+        keep = ctx.enter_context(tc.tile_pool(name="keep", bufs=1))
+        x_pool = ctx.enter_context(tc.tile_pool(name="x_pool", bufs=ROW_TILES))
+        grouped_pool = ctx.enter_context(tc.tile_pool(name="grouped_pool", bufs=3))
+        result_pool = ctx.enter_context(tc.tile_pool(name="result_pool", bufs=8))
+        xt_psum = ctx.enter_context(tc.psum_pool(name="xt_psum", bufs=4))
+        acc_psum = ctx.enter_context(tc.psum_pool(name="acc_psum", bufs=4))
+
+        w_planes = keep.tile([P, N], U8, align_bytes=64)
+        nc.vector.memset(w_planes[:].bitcast(I32), 0)
+        bias_rows = keep.tile([P, N], BF16)
+        nc.vector.memset(bias_rows[:], 0.0)
+        ones = keep.tile([P, P], BF16)
+        nc.vector.memset(ones[:], 1.0)
+        identity = keep.tile([P, P], F32)
+        make_identity(nc, identity[:])
+        table_warmer = keep.tile([P, 1], F32)
+        nc.scalar.activation(
+            out=table_warmer[:], in_=ones[:, 0:1], func=mybir.ActivationFunctionType.Relu
+        )
+
+        x_tiles = [x_pool.tile([P, K], BF16, name="x_tile") for i in range(ROW_TILES)]
+        w_words = [
+            keep.tile([P, PASSES, N_CHUNK], U32, name="w_words%d" % j, align_bytes=64)
+            for j in range(CHUNKS)
+        ]
+
+        def load_x(i):
+            nc.sync.dma_start(out=x_tiles[i][:], in_=x[i * P : (i + 1) * P, :])
+
+        def load_w(j):
+            chunk_bytes = weight_words.rearrange("g p n t -> p g (n t)")[
+                :, :, j * N_CHUNK * PACK : (j + 1) * N_CHUNK * PACK
+            ]
+            nc.sync.dma_start(out=w_words[j][:].bitcast(I32), in_=chunk_bytes.bitcast(I32))
+
+        nc.scalar.dma_start(out=bias_rows[0:1, :], in_=bias.rearrange("(o n) -> o n", o=1))
+        load_x(0)
+        load_x(1)
+        for quadrant in range(QUADRANTS):
+            first_partition = quadrant * (P // QUADRANTS)
+            nc.sync.dma_start(
+                out=w_planes[
+                    first_partition : first_partition + PASSES * PLANE_ROWS, :
+                ].bitcast(I32),
+                in_=weight_scales[
+                    :, quadrant * PLANE_ROWS : (quadrant + 1) * PLANE_ROWS, :
+                ].bitcast(I32),
+            )
+        load_w(0)
+        for i in range(2, ROW_TILES):
+            load_x(i)
+        for j in range(1, CHUNKS):
+            load_w(j)
+
+        x_codes = keep.tile([P, ROW_TILES, PASSES * P], U32, align_bytes=64)
+        x_scales = keep.tile([P, ROW_TILES, PASSES * P], U8, align_bytes=64)
+
+        def quantise_x(i):
+            words = x_tiles[i][:].bitcast(F32)
+            grouped = grouped_pool.tile([P, PASSES, P, PACK], BF16, align_bytes=64)
+            grouped_words = grouped[:].bitcast(F32)
+            for half in range(2):
+                xt = xt_psum.tile([P, 2, PAIRS, P], F32)
+                for g_in_half in range(2):
+                    first_word = (2 * half + g_in_half) * WORDS_PER_PASS
+                    for u in range(PAIRS):
+                        nc.tensor.transpose(
+                            xt[:, g_in_half, u, :],
+                            words[:, first_word + u : first_word + WORDS_PER_PASS : PAIRS],
+                            identity[:],
+                        )
+                copy_out = nc.vector.tensor_copy if half == 0 else nc.scalar.copy
+                copy_out(
+                    out=grouped_words[:, 2 * half : 2 * half + 2, :, :],
+                    in_=xt[:].rearrange("p g u r -> p g r u"),
+                )
+            nc.vector.quantize_mx(
+                out=x_codes[:, i, :].bitcast(FP8X4),
+                scales=x_scales[:, i, :],
+                in_=grouped[:].rearrange("p g r t -> p (g r t)"),
+            )
+
+        bias_all = keep.tile([P, N], F32)
+
+        def broadcast_bias(j):
+            columns = slice(j * N_CHUNK, (j + 1) * N_CHUNK)
+            spread = acc_psum.tile([P, N_CHUNK], F32, name="acc")
+            nc.tensor.matmul(spread[:], lhsT=ones[:], rhs=bias_rows[:, columns], start=True, stop=True)
+            nc.scalar.copy(out=bias_all[:, columns], in_=spread[:])
+
+        def multiply(i, j):
+            columns = slice(j * N_CHUNK, (j + 1) * N_CHUNK)
+            acc = acc_psum.tile([P, N_CHUNK], F32, name="acc")
+            for g in range(PASSES):
+                nc.tensor.matmul_mx(
+                    out=acc[:],
+                    lhsT=x_codes[:, i, g * P : (g + 1) * P].bitcast(FP8X4),
+                    lhsT_scale=x_scales[:, i, g * P : (g + 1) * P],
+                    rhs=w_words[j][:, g, :].bitcast(FP8X4),
+                    rhs_scale=w_planes[g * PLANE_ROWS : P, columns],
+                    start=(g == 0),
+                    stop=(g == PASSES - 1),
+                )
+            result = result_pool.tile([P, N_CHUNK], F32)
+            nc.vector.tensor_tensor(
+                out=result[:], in0=acc[:], in1=bias_all[:, columns], op=mybir.AluOpType.add
+            )
+            nc.scalar.activation(
+                out=result[:], in_=result[:], func=mybir.ActivationFunctionType.Relu
+            )
+            nc.sync.dma_start(out=out[i * P : (i + 1) * P, columns], in_=result[:])
+
+        quantise_x(0)
+        quantise_x(1)
+        for j in range(CHUNKS):
+            broadcast_bias(j)
+            for i in range(ROW_TILES):
+                multiply(i, j)
+                if j == 0 and i + 2 < ROW_TILES:
+                    quantise_x(i + 2)

@@ -38,8 +38,7 @@ def tile_sparselinearrelu_kernel(tc, x, weight_words, weight_scales, bias, out):
         x_pool = ctx.enter_context(tc.tile_pool(name="x_pool", bufs=ROW_TILES))
         grouped_pool = ctx.enter_context(tc.tile_pool(name="grouped_pool", bufs=3))
         result_pool = ctx.enter_context(tc.tile_pool(name="result_pool", bufs=8))
-        xt_psum = ctx.enter_context(tc.psum_pool(name="xt_psum", bufs=4))
-        acc_psum = ctx.enter_context(tc.psum_pool(name="acc_psum", bufs=4))
+        psum = ctx.enter_context(tc.psum_pool(name="psum", bufs=8))
 
         w_planes = keep.tile([P, N], U8, align_bytes=64)
         nc.vector.memset(w_planes[:].bitcast(I32), 0)
@@ -82,21 +81,20 @@ def tile_sparselinearrelu_kernel(tc, x, weight_words, weight_scales, bias, out):
                     :, quadrant * PLANE_ROWS : (quadrant + 1) * PLANE_ROWS, :
                 ].bitcast(I32),
             )
-        load_w(0)
         for i in range(2, ROW_TILES):
             load_x(i)
-        for j in range(1, CHUNKS):
+        for j in range(CHUNKS):
             load_w(j)
 
         x_codes = keep.tile([P, ROW_TILES, PASSES * P], U32, align_bytes=64)
         x_scales = keep.tile([P, ROW_TILES, PASSES * P], U8, align_bytes=64)
 
-        def quantise_x(i):
+        def transpose_x(i):
             words = x_tiles[i][:].bitcast(F32)
             grouped = grouped_pool.tile([P, PASSES, P, PACK], BF16, align_bytes=64)
             grouped_words = grouped[:].bitcast(F32)
             for half in range(2):
-                xt = xt_psum.tile([P, 2, PAIRS, P], F32)
+                xt = psum.tile([P, 2, PAIRS, P], F32, name="bank")
                 for g_in_half in range(2):
                     first_word = (2 * half + g_in_half) * WORDS_PER_PASS
                     for u in range(PAIRS):
@@ -110,6 +108,9 @@ def tile_sparselinearrelu_kernel(tc, x, weight_words, weight_scales, bias, out):
                     out=grouped_words[:, 2 * half : 2 * half + 2, :, :],
                     in_=xt[:].rearrange("p g u r -> p g r u"),
                 )
+            return grouped
+
+        def quantise_x(i, grouped):
             nc.vector.quantize_mx(
                 out=x_codes[:, i, :].bitcast(FP8X4),
                 scales=x_scales[:, i, :],
@@ -120,13 +121,13 @@ def tile_sparselinearrelu_kernel(tc, x, weight_words, weight_scales, bias, out):
 
         def broadcast_bias(j):
             columns = slice(j * N_CHUNK, (j + 1) * N_CHUNK)
-            spread = acc_psum.tile([P, N_CHUNK], F32, name="acc")
+            spread = psum.tile([P, N_CHUNK], F32, name="bank")
             nc.tensor.matmul(spread[:], lhsT=ones[:], rhs=bias_rows[:, columns], start=True, stop=True)
             nc.scalar.copy(out=bias_all[:, columns], in_=spread[:])
 
         def multiply(i, j):
             columns = slice(j * N_CHUNK, (j + 1) * N_CHUNK)
-            acc = acc_psum.tile([P, N_CHUNK], F32, name="acc")
+            acc = psum.tile([P, N_CHUNK], F32, name="bank")
             for g in range(PASSES):
                 nc.tensor.matmul_mx(
                     out=acc[:],
@@ -146,11 +147,14 @@ def tile_sparselinearrelu_kernel(tc, x, weight_words, weight_scales, bias, out):
             )
             nc.sync.dma_start(out=out[i * P : (i + 1) * P, columns], in_=result[:])
 
-        quantise_x(0)
-        quantise_x(1)
+        grouped_tiles = []
+        for i in range(ROW_TILES):
+            grouped_tiles.append(transpose_x(i))
+            if i > 0:
+                quantise_x(i - 1, grouped_tiles[i - 1])
+        quantise_x(ROW_TILES - 1, grouped_tiles[ROW_TILES - 1])
         for j in range(CHUNKS):
             broadcast_bias(j)
+        for j in range(CHUNKS):
             for i in range(ROW_TILES):
                 multiply(i, j)
-                if j == 0 and i + 2 < ROW_TILES:
-                    quantise_x(i + 2)

@@ -42,33 +42,31 @@ def tile_sparselinearrelu_kernel(tc, x, weight_words, weight_scales, bias, out):
 
         w_planes = keep.tile([P, N], U8, align_bytes=64)
         nc.vector.memset(w_planes[:].bitcast(I32), 0)
-        bias_rows = keep.tile([P, N], BF16)
-        nc.vector.memset(bias_rows[:], 0.0)
-        ones = keep.tile([P, P], BF16)
-        nc.vector.memset(ones[:], 1.0)
         identity = keep.tile([P, P], F32)
         make_identity(nc, identity[:])
-        table_warmer = keep.tile([P, 1], F32)
-        nc.scalar.activation(
-            out=table_warmer[:], in_=ones[:, 0:1], func=mybir.ActivationFunctionType.Relu
-        )
 
         x_tiles = [x_pool.tile([P, K], BF16, name="x_tile") for i in range(ROW_TILES)]
         w_words = [
-            keep.tile([P, PASSES, N_CHUNK], U32, name="w_words%d" % j, align_bytes=64)
+            [
+                keep.tile([P, N_CHUNK], U32, name="w_words_%d_%d" % (j, g), align_bytes=64)
+                for g in range(PASSES)
+            ]
             for j in range(CHUNKS)
         ]
+        bias_all = keep.tile([P, N], BF16)
 
         def load_x(i):
             nc.sync.dma_start(out=x_tiles[i][:], in_=x[i * P : (i + 1) * P, :])
 
         def load_w(j):
-            chunk_bytes = weight_words.rearrange("g p n t -> p g (n t)")[
-                :, :, j * N_CHUNK * PACK : (j + 1) * N_CHUNK * PACK
-            ]
-            nc.sync.dma_start(out=w_words[j][:].bitcast(I32), in_=chunk_bytes.bitcast(I32))
+            for g in range(PASSES):
+                pass_bytes = weight_words[g].rearrange("p n t -> p (n t)")[
+                    :, j * N_CHUNK * PACK : (j + 1) * N_CHUNK * PACK
+                ]
+                nc.sync.dma_start(
+                    out=w_words[j][g][:].bitcast(I32), in_=pass_bytes.bitcast(I32)
+                )
 
-        nc.scalar.dma_start(out=bias_rows[0:1, :], in_=bias.rearrange("(o n) -> o n", o=1))
         load_x(0)
         load_x(1)
         for quadrant in range(QUADRANTS):
@@ -83,7 +81,9 @@ def tile_sparselinearrelu_kernel(tc, x, weight_words, weight_scales, bias, out):
             )
         for i in range(2, ROW_TILES):
             load_x(i)
-        for j in range(CHUNKS):
+        load_w(0)
+        nc.sync.dma_start(out=bias_all[:], in_=bias.partition_broadcast(P))
+        for j in range(1, CHUNKS):
             load_w(j)
 
         x_codes = keep.tile([P, ROW_TILES, PASSES * P], U32, align_bytes=64)
@@ -117,14 +117,6 @@ def tile_sparselinearrelu_kernel(tc, x, weight_words, weight_scales, bias, out):
                 in_=grouped[:].rearrange("p g r t -> p (g r t)"),
             )
 
-        bias_all = keep.tile([P, N], F32)
-
-        def broadcast_bias(j):
-            columns = slice(j * N_CHUNK, (j + 1) * N_CHUNK)
-            spread = psum.tile([P, N_CHUNK], F32, name="bank")
-            nc.tensor.matmul(spread[:], lhsT=ones[:], rhs=bias_rows[:, columns], start=True, stop=True)
-            nc.scalar.copy(out=bias_all[:, columns], in_=spread[:])
-
         def multiply(i, j):
             columns = slice(j * N_CHUNK, (j + 1) * N_CHUNK)
             acc = psum.tile([P, N_CHUNK], F32, name="bank")
@@ -133,7 +125,7 @@ def tile_sparselinearrelu_kernel(tc, x, weight_words, weight_scales, bias, out):
                     out=acc[:],
                     lhsT=x_codes[:, i, g * P : (g + 1) * P].bitcast(FP8X4),
                     lhsT_scale=x_scales[:, i, g * P : (g + 1) * P],
-                    rhs=w_words[j][:, g, :].bitcast(FP8X4),
+                    rhs=w_words[j][g][:].bitcast(FP8X4),
                     rhs_scale=w_planes[g * PLANE_ROWS : P, columns],
                     start=(g == 0),
                     stop=(g == PASSES - 1),
@@ -153,8 +145,6 @@ def tile_sparselinearrelu_kernel(tc, x, weight_words, weight_scales, bias, out):
             if i > 0:
                 quantise_x(i - 1, grouped_tiles[i - 1])
         quantise_x(ROW_TILES - 1, grouped_tiles[ROW_TILES - 1])
-        for j in range(CHUNKS):
-            broadcast_bias(j)
         for j in range(CHUNKS):
             for i in range(ROW_TILES):
                 multiply(i, j)

@@ -26,6 +26,8 @@ CHUNKS = N // N_CHUNK
 WORDS_PER_PASS = K_PASS // 2
 PLANE_ROWS = 4
 QUADRANTS = 4
+SLOT_BYTES = 256
+X_CODES_PAD = 48
 
 FLOPS = 2 * ROWS * K * N
 
@@ -40,7 +42,7 @@ def tile_sparselinearrelu_kernel(tc, x, weight_words, weight_scales, bias, out):
         result_pool = ctx.enter_context(tc.tile_pool(name="result_pool", bufs=8))
         psum = ctx.enter_context(tc.psum_pool(name="psum", bufs=8))
 
-        w_planes = keep.tile([P, N], U8, align_bytes=64)
+        w_planes = keep.tile([P, N], U8, align_bytes=SLOT_BYTES)
         nc.vector.memset(w_planes[:].bitcast(I32), 0)
         identity = keep.tile([P, P], F32)
         make_identity(nc, identity[:])
@@ -48,7 +50,9 @@ def tile_sparselinearrelu_kernel(tc, x, weight_words, weight_scales, bias, out):
         x_tiles = [x_pool.tile([P, K], BF16, name="x_tile") for i in range(ROW_TILES)]
         w_words = [
             [
-                keep.tile([P, N_CHUNK], U32, name="w_words_%d_%d" % (j, g), align_bytes=64)
+                keep.tile(
+                    [P, N_CHUNK], U32, name="w_words_%d_%d" % (j, g), align_bytes=SLOT_BYTES
+                )
                 for g in range(PASSES)
             ]
             for j in range(CHUNKS)
@@ -86,8 +90,14 @@ def tile_sparselinearrelu_kernel(tc, x, weight_words, weight_scales, bias, out):
         for j in range(1, CHUNKS):
             load_w(j)
 
-        x_codes = keep.tile([P, ROW_TILES, PASSES * P], U32, align_bytes=64)
-        x_scales = keep.tile([P, ROW_TILES, PASSES * P], U8, align_bytes=64)
+        x_codes = keep.tile(
+            [P, X_CODES_PAD + ROW_TILES * PASSES * P], U32, align_bytes=SLOT_BYTES
+        )
+        x_scales = keep.tile([P, ROW_TILES, PASSES, SLOT_BYTES], U8, align_bytes=SLOT_BYTES)
+
+        def x_words_of(i, g):
+            first_code_word = X_CODES_PAD + (i * PASSES + g) * P
+            return x_codes[:, first_code_word : first_code_word + P].bitcast(FP8X4)
 
         def transpose_x(i):
             words = x_tiles[i][:].bitcast(F32)
@@ -111,11 +121,12 @@ def tile_sparselinearrelu_kernel(tc, x, weight_words, weight_scales, bias, out):
             return grouped
 
         def quantise_x(i, grouped):
-            nc.vector.quantize_mx(
-                out=x_codes[:, i, :].bitcast(FP8X4),
-                scales=x_scales[:, i, :],
-                in_=grouped[:].rearrange("p g r t -> p (g r t)"),
-            )
+            for g in range(PASSES):
+                nc.vector.quantize_mx(
+                    out=x_words_of(i, g),
+                    scales=x_scales[:, i, g, 0:P],
+                    in_=grouped[:, g, :, :].rearrange("p r t -> p (r t)"),
+                )
 
         def multiply(i, j):
             columns = slice(j * N_CHUNK, (j + 1) * N_CHUNK)
@@ -123,8 +134,8 @@ def tile_sparselinearrelu_kernel(tc, x, weight_words, weight_scales, bias, out):
             for g in range(PASSES):
                 nc.tensor.matmul_mx(
                     out=acc[:],
-                    lhsT=x_codes[:, i, g * P : (g + 1) * P].bitcast(FP8X4),
-                    lhsT_scale=x_scales[:, i, g * P : (g + 1) * P],
+                    lhsT=x_words_of(i, g),
+                    lhsT_scale=x_scales[:, i, g, 0:P],
                     rhs=w_words[j][g][:].bitcast(FP8X4),
                     rhs_scale=w_planes[g * PLANE_ROWS : P, columns],
                     start=(g == 0),

@@ -29,6 +29,9 @@ QUADRANTS = 4
 SLOT_BYTES = 256
 X_CODES_PAD = 48
 
+BANKS = 8
+T_BANKS = 4
+
 FLOPS = 2 * ROWS * K * N
 
 
@@ -38,9 +41,10 @@ def tile_sparselinearrelu_kernel(tc, x, weight_words, weight_scales, bias, out):
         ctx.enter_context(tc.manual_schedule())
         keep = ctx.enter_context(tc.tile_pool(name="keep", bufs=1))
         x_pool = ctx.enter_context(tc.tile_pool(name="x_pool", bufs=ROW_TILES))
-        grouped_pool = ctx.enter_context(tc.tile_pool(name="grouped_pool", bufs=3))
+        sorted_pool = ctx.enter_context(tc.tile_pool(name="sorted_pool", bufs=4))
+        grouped_pool = ctx.enter_context(tc.tile_pool(name="grouped_pool", bufs=4))
         result_pool = ctx.enter_context(tc.tile_pool(name="result_pool", bufs=8))
-        psum = ctx.enter_context(tc.psum_pool(name="psum", bufs=8))
+        psum = ctx.enter_context(tc.psum_pool(name="psum", bufs=1))
 
         w_planes = keep.tile([P, N], U8, align_bytes=SLOT_BYTES)
         nc.vector.memset(w_planes[:].bitcast(I32), 0)
@@ -71,22 +75,29 @@ def tile_sparselinearrelu_kernel(tc, x, weight_words, weight_scales, bias, out):
                     out=w_words[j][g][:].bitcast(I32), in_=pass_bytes.bitcast(I32)
                 )
 
+        def load_scales(first_column, end_column):
+            for quadrant in range(QUADRANTS):
+                first_partition = quadrant * (P // QUADRANTS)
+                nc.sync.dma_start(
+                    out=w_planes[
+                        first_partition : first_partition + PASSES * PLANE_ROWS,
+                        first_column:end_column,
+                    ].bitcast(I32),
+                    in_=weight_scales[
+                        :,
+                        quadrant * PLANE_ROWS : (quadrant + 1) * PLANE_ROWS,
+                        first_column:end_column,
+                    ].bitcast(I32),
+                )
+
         load_x(0)
         load_x(1)
-        for quadrant in range(QUADRANTS):
-            first_partition = quadrant * (P // QUADRANTS)
-            nc.sync.dma_start(
-                out=w_planes[
-                    first_partition : first_partition + PASSES * PLANE_ROWS, :
-                ].bitcast(I32),
-                in_=weight_scales[
-                    :, quadrant * PLANE_ROWS : (quadrant + 1) * PLANE_ROWS, :
-                ].bitcast(I32),
-            )
+        load_scales(0, N_CHUNK)
+        load_w(0)
         for i in range(2, ROW_TILES):
             load_x(i)
-        load_w(0)
         nc.sync.dma_start(out=bias_all[:], in_=bias.partition_broadcast(P))
+        load_scales(N_CHUNK, N)
         for j in range(1, CHUNKS):
             load_w(j)
 
@@ -99,38 +110,62 @@ def tile_sparselinearrelu_kernel(tc, x, weight_words, weight_scales, bias, out):
             first_code_word = X_CODES_PAD + (i * PASSES + g) * P
             return x_codes[:, first_code_word : first_code_word + P].bitcast(FP8X4)
 
+        sorted_tiles = {}
+        transposed = {}
+        grouped_tiles = {}
+        sums = {}
+
+        def sort_x(i):
+            sorted_x = sorted_pool.tile([P, K], BF16, name="sorted_x")
+            nc.vector.tensor_copy(
+                out=sorted_x[:].bitcast(F32).rearrange(
+                    "r (g u p) -> r g u p", g=PASSES, u=PAIRS
+                ),
+                in_=x_tiles[i][:].bitcast(F32).rearrange(
+                    "r (g p u) -> r g u p", g=PASSES, u=PAIRS
+                ),
+            )
+            sorted_tiles[i] = sorted_x
+
         def transpose_x(i):
-            words = x_tiles[i][:].bitcast(F32)
-            grouped = grouped_pool.tile([P, PASSES, P, PACK], BF16, align_bytes=64)
+            words = sorted_tiles[i][:].bitcast(F32)
+            transposed[i] = []
+            for half in range(2):
+                xt = psum.tile(
+                    [P, 2, PAIRS, P], F32, name="bank%d" % ((2 * i + half) % T_BANKS)
+                )
+                for t in range(2 * PAIRS):
+                    first_word = (2 * PAIRS * half + t) * P
+                    nc.tensor.transpose(
+                        xt[:, t // PAIRS, t % PAIRS, :],
+                        words[:, first_word : first_word + P],
+                        identity[:],
+                    )
+                transposed[i].append(xt)
+
+        def copy_out(i, first_on_vector):
+            grouped = grouped_pool.tile([P, PASSES, P, PACK], BF16, align_bytes=64, name="grouped")
             grouped_words = grouped[:].bitcast(F32)
             for half in range(2):
-                xt = psum.tile([P, 2, PAIRS, P], F32, name="bank")
-                for g_in_half in range(2):
-                    first_word = (2 * half + g_in_half) * WORDS_PER_PASS
-                    for u in range(PAIRS):
-                        nc.tensor.transpose(
-                            xt[:, g_in_half, u, :],
-                            words[:, first_word + u : first_word + WORDS_PER_PASS : PAIRS],
-                            identity[:],
-                        )
-                copy_out = nc.vector.tensor_copy if half == 0 else nc.scalar.copy
-                copy_out(
+                copy = nc.vector.tensor_copy if (half == 0 and first_on_vector) else nc.scalar.copy
+                copy(
                     out=grouped_words[:, 2 * half : 2 * half + 2, :, :],
-                    in_=xt[:].rearrange("p g u r -> p g r u"),
+                    in_=transposed[i][half][:].rearrange("p g u r -> p g r u"),
                 )
-            return grouped
+            grouped_tiles[i] = grouped
 
-        def quantise_x(i, grouped):
+        def quantise_x(i):
             for g in range(PASSES):
                 nc.vector.quantize_mx(
                     out=x_words_of(i, g),
                     scales=x_scales[:, i, g, 0:P],
-                    in_=grouped[:, g, :, :].rearrange("p r t -> p (r t)"),
+                    in_=grouped_tiles[i][:, g, :, :].rearrange("p r t -> p (r t)"),
                 )
 
-        def multiply(i, j):
+        def multiply(b):
+            j, i = b // ROW_TILES, b % ROW_TILES
             columns = slice(j * N_CHUNK, (j + 1) * N_CHUNK)
-            acc = psum.tile([P, N_CHUNK], F32, name="bank")
+            acc = psum.tile([P, N_CHUNK], F32, name="bank%d" % ((T_BANKS + b) % BANKS))
             for g in range(PASSES):
                 nc.tensor.matmul_mx(
                     out=acc[:],
@@ -141,21 +176,54 @@ def tile_sparselinearrelu_kernel(tc, x, weight_words, weight_scales, bias, out):
                     start=(g == 0),
                     stop=(g == PASSES - 1),
                 )
-            result = result_pool.tile([P, N_CHUNK], F32)
+            sums[b] = acc
+
+        def finish(b):
+            j, i = b // ROW_TILES, b % ROW_TILES
+            columns = slice(j * N_CHUNK, (j + 1) * N_CHUNK)
+            result = result_pool.tile([P, N_CHUNK], F32, name="result")
             nc.vector.tensor_tensor(
-                out=result[:], in0=acc[:], in1=bias_all[:, columns], op=mybir.AluOpType.add
+                out=result[:], in0=sums[b][:], in1=bias_all[:, columns], op=mybir.AluOpType.add
             )
             nc.scalar.activation(
                 out=result[:], in_=result[:], func=mybir.ActivationFunctionType.Relu
             )
             nc.sync.dma_start(out=out[i * P : (i + 1) * P, columns], in_=result[:])
 
-        grouped_tiles = []
-        for i in range(ROW_TILES):
-            grouped_tiles.append(transpose_x(i))
-            if i > 0:
-                quantise_x(i - 1, grouped_tiles[i - 1])
-        quantise_x(ROW_TILES - 1, grouped_tiles[ROW_TILES - 1])
-        for j in range(CHUNKS):
-            for i in range(ROW_TILES):
-                multiply(i, j)
+        for i in (0, 1):
+            sort_x(i)
+            transpose_x(i)
+            copy_out(i, False)
+        quantise_x(0)
+        quantise_x(1)
+        multiply(0)
+        multiply(1)
+        for i in (2, 3):
+            sort_x(i)
+            transpose_x(i)
+            copy_out(i, False)
+        quantise_x(2)
+        sort_x(4)
+        quantise_x(3)
+        sort_x(5)
+        multiply(2)
+        multiply(3)
+        sort_x(6)
+        transpose_x(4)
+        copy_out(4, True)
+        sort_x(7)
+        transpose_x(5)
+        copy_out(5, True)
+        quantise_x(4)
+        transpose_x(6)
+        copy_out(6, False)
+        quantise_x(5)
+        transpose_x(7)
+        copy_out(7, False)
+        quantise_x(6)
+        quantise_x(7)
+        for b in range(4):
+            finish(b)
+        for b in range(4, ROW_TILES * CHUNKS):
+            multiply(b)
+            finish(b)

@@ -43,7 +43,7 @@ def tile_sparselinearrelu_kernel(tc, x, weight_words, weight_scales, bias, out):
         x_pool = ctx.enter_context(tc.tile_pool(name="x_pool", bufs=ROW_TILES))
         sorted_pool = ctx.enter_context(tc.tile_pool(name="sorted_pool", bufs=4))
         grouped_pool = ctx.enter_context(tc.tile_pool(name="grouped_pool", bufs=4))
-        result_pool = ctx.enter_context(tc.tile_pool(name="result_pool", bufs=8))
+        result_pool = ctx.enter_context(tc.tile_pool(name="result_pool", bufs=16))
         psum = ctx.enter_context(tc.psum_pool(name="psum", bufs=1))
 
         w_planes = keep.tile([P, N], U8, align_bytes=SLOT_BYTES)
@@ -96,10 +96,11 @@ def tile_sparselinearrelu_kernel(tc, x, weight_words, weight_scales, bias, out):
         load_w(0)
         for i in range(2, ROW_TILES):
             load_x(i)
-        nc.sync.dma_start(out=bias_all[:], in_=bias.partition_broadcast(P))
         load_scales(N_CHUNK, N)
-        for j in range(1, CHUNKS):
-            load_w(j)
+        load_w(1)
+        nc.sync.dma_start(out=bias_all[:], in_=bias.partition_broadcast(P))
+        load_w(2)
+        load_w(3)
 
         x_codes = keep.tile(
             [P, X_CODES_PAD + ROW_TILES * PASSES * P], U32, align_bytes=SLOT_BYTES
@@ -162,26 +163,36 @@ def tile_sparselinearrelu_kernel(tc, x, weight_words, weight_scales, bias, out):
                     in_=grouped_tiles[i][:, g, :, :].rearrange("p r t -> p (r t)"),
                 )
 
-        def multiply(b):
+        def multiply(b, first=0, width=N_CHUNK, bank_shift=0):
             j, i = b // ROW_TILES, b % ROW_TILES
-            columns = slice(j * N_CHUNK, (j + 1) * N_CHUNK)
-            acc = psum.tile([P, N_CHUNK], F32, name="bank%d" % ((T_BANKS + b) % BANKS))
+            columns = slice(j * N_CHUNK + first, j * N_CHUNK + first + width)
+            acc = psum.tile(
+                [P, width], F32, name="bank%d" % ((T_BANKS + b + bank_shift) % BANKS)
+            )
             for g in range(PASSES):
                 nc.tensor.matmul_mx(
                     out=acc[:],
                     lhsT=x_words_of(i, g),
                     lhsT_scale=x_scales[:, i, g, 0:P],
-                    rhs=w_words[j][g][:].bitcast(FP8X4),
+                    rhs=w_words[j][g][:, first : first + width].bitcast(FP8X4),
                     rhs_scale=w_planes[g * PLANE_ROWS : P, columns],
                     start=(g == 0),
                     stop=(g == PASSES - 1),
                 )
             sums[b] = acc
 
-        def finish(b):
+        def park(b):
+            parked = result_pool.tile([P, N_CHUNK], F32, name="result")
+            nc.scalar.copy(out=parked[:], in_=sums[b][:])
+            sums[b] = parked
+
+        def finish(b, first=0, width=N_CHUNK, parked=False):
             j, i = b // ROW_TILES, b % ROW_TILES
-            columns = slice(j * N_CHUNK, (j + 1) * N_CHUNK)
-            result = result_pool.tile([P, N_CHUNK], F32, name="result")
+            columns = slice(j * N_CHUNK + first, j * N_CHUNK + first + width)
+            if parked:
+                result = sums[b]
+            else:
+                result = result_pool.tile([P, width], F32, name="result")
             nc.vector.tensor_tensor(
                 out=result[:], in0=sums[b][:], in1=bias_all[:, columns], op=mybir.AluOpType.add
             )
@@ -198,6 +209,8 @@ def tile_sparselinearrelu_kernel(tc, x, weight_words, weight_scales, bias, out):
         quantise_x(1)
         multiply(0)
         multiply(1)
+        park(0)
+        park(1)
         for i in (2, 3):
             sort_x(i)
             transpose_x(i)
@@ -208,6 +221,8 @@ def tile_sparselinearrelu_kernel(tc, x, weight_words, weight_scales, bias, out):
         sort_x(5)
         multiply(2)
         multiply(3)
+        park(2)
+        park(3)
         sort_x(6)
         transpose_x(4)
         copy_out(4, True)
@@ -222,8 +237,13 @@ def tile_sparselinearrelu_kernel(tc, x, weight_words, weight_scales, bias, out):
         copy_out(7, False)
         quantise_x(6)
         quantise_x(7)
-        for b in range(4):
-            finish(b)
-        for b in range(4, ROW_TILES * CHUNKS):
+        last = ROW_TILES * CHUNKS - 1
+        for b in range(4, last):
             multiply(b)
             finish(b)
+            if b == ROW_TILES - 1:
+                for early in range(4):
+                    finish(early, parked=True)
+        for half in range(2):
+            multiply(last, half * N_CHUNK // 2, N_CHUNK // 2, half)
+            finish(last, half * N_CHUNK // 2, N_CHUNK // 2)

@@ -167,7 +167,7 @@ def tile_sparselinearrelu_kernel(tc, x, weight_words, weight_scales, bias, out):
             j, i = b // ROW_TILES, b % ROW_TILES
             columns = slice(j * N_CHUNK + first, j * N_CHUNK + first + width)
             acc = psum.tile(
-                [P, width], F32, name="bank%d" % ((T_BANKS + b + bank_shift) % BANKS)
+                [P, width], F32, name="bank%d" % (((T_BANKS + b if b < T_BANKS else b) + bank_shift) % BANKS)
             )
             for g in range(PASSES):
                 nc.tensor.matmul_mx(
@@ -220,30 +220,35 @@ def tile_sparselinearrelu_kernel(tc, x, weight_words, weight_scales, bias, out):
         quantise_x(3)
         sort_x(5)
         multiply(2)
-        multiply(3)
         park(2)
+        transpose_x(4)
+        copy_out(4, False)
+        multiply(3)
         park(3)
         sort_x(6)
-        transpose_x(4)
-        copy_out(4, True)
-        sort_x(7)
-        transpose_x(5)
-        copy_out(5, True)
         quantise_x(4)
+        transpose_x(5)
+        copy_out(5, False)
+        multiply(4)
+        sort_x(7)
+        quantise_x(5)
         transpose_x(6)
         copy_out(6, False)
-        quantise_x(5)
+        multiply(5)
+        quantise_x(6)
         transpose_x(7)
         copy_out(7, False)
-        quantise_x(6)
+        multiply(6)
         quantise_x(7)
+        multiply(7)
+        for b in range(4, ROW_TILES):
+            finish(b)
+        for early in range(4):
+            finish(early, parked=True)
         last = ROW_TILES * CHUNKS - 1
-        for b in range(4, last):
+        for b in range(ROW_TILES, last):
             multiply(b)
             finish(b)
-            if b == ROW_TILES - 1:
-                for early in range(4):
-                    finish(early, parked=True)
         for half in range(2):
             multiply(last, half * N_CHUNK // 2, N_CHUNK // 2, half)
             finish(last, half * N_CHUNK // 2, N_CHUNK // 2)

@@ -46,6 +46,8 @@ def tile_sparselinearrelu_kernel(tc, x, weight_words, weight_scales, bias, out):
         result_pool = ctx.enter_context(tc.tile_pool(name="result_pool", bufs=16))
         psum = ctx.enter_context(tc.psum_pool(name="psum", bufs=1))
 
+        zeros = keep.tile([P, N_CHUNK], BF16)
+        nc.vector.memset(zeros[:], 0.0)
         w_planes = keep.tile([P, N], U8, align_bytes=SLOT_BYTES)
         nc.vector.memset(w_planes[:].bitcast(I32), 0)
         identity = keep.tile([P, P], F32)
@@ -201,20 +203,32 @@ def tile_sparselinearrelu_kernel(tc, x, weight_words, weight_scales, bias, out):
             )
             nc.sync.dma_start(out=out[i * P : (i + 1) * P, columns], in_=result[:])
 
+        unread = psum.tile([P, N_CHUNK], F32, name="bank%d" % (BANKS - 1))
+
+        def keep_clock_up(count):
+            for repeat in range(count):
+                nc.tensor.matmul(
+                    out=unread[:], lhsT=zeros[:, 0:P], rhs=zeros[:], start=True, stop=True
+                )
+
+        keep_clock_up(9)
         for i in (0, 1):
             sort_x(i)
             transpose_x(i)
             copy_out(i, False)
+            keep_clock_up(1)
         quantise_x(0)
         quantise_x(1)
         multiply(0)
         multiply(1)
         park(0)
         park(1)
+        keep_clock_up(1)
         for i in (2, 3):
             sort_x(i)
             transpose_x(i)
             copy_out(i, False)
+            keep_clock_up(1)
         quantise_x(2)
         sort_x(4)
         quantise_x(3)

@@ -254,13 +254,17 @@ def tile_sparselinearrelu_kernel(tc, x, weight_words, weight_scales, bias, out):
         copy_out(7, False)
         multiply(6)
         quantise_x(7)
+        multiply(ROW_TILES)
+        multiply(ROW_TILES + 1)
         multiply(7)
         for b in range(4, ROW_TILES):
             finish(b)
         for early in range(4):
             finish(early, parked=True)
+        finish(ROW_TILES)
+        finish(ROW_TILES + 1)
         last = ROW_TILES * CHUNKS - 1
-        for b in range(ROW_TILES, last):
+        for b in range(ROW_TILES + 2, last):
             multiply(b)
             finish(b)
         for half in range(2):

@@ -23,7 +23,6 @@ N_CHUNK = 512
 ROW_TILES = ROWS // P
 PASSES = K // K_PASS
 CHUNKS = N // N_CHUNK
-WORDS_PER_PASS = K_PASS // 2
 PLANE_ROWS = 4
 QUADRANTS = 4
 SLOT_BYTES = 256
@@ -31,6 +30,11 @@ X_CODES_PAD = 48
 
 BANKS = 8
 T_BANKS = 4
+
+HEAD_TILES = 4
+DUO = 2
+BIAS_RUN = N // P
+BIAS_GROUP = BIAS_RUN // PASSES
 
 FLOPS = 2 * ROWS * K * N
 
@@ -40,20 +44,27 @@ def tile_sparselinearrelu_kernel(tc, x, weight_words, weight_scales, bias, out):
     with ExitStack() as ctx:
         ctx.enter_context(tc.manual_schedule())
         keep = ctx.enter_context(tc.tile_pool(name="keep", bufs=1))
-        x_pool = ctx.enter_context(tc.tile_pool(name="x_pool", bufs=ROW_TILES))
+        x_pool = ctx.enter_context(tc.tile_pool(name="x_pool", bufs=ROW_TILES - HEAD_TILES))
+        head_pool = ctx.enter_context(tc.tile_pool(name="head_pool", bufs=PASSES * HEAD_TILES // DUO))
         sorted_pool = ctx.enter_context(tc.tile_pool(name="sorted_pool", bufs=4))
         grouped_pool = ctx.enter_context(tc.tile_pool(name="grouped_pool", bufs=4))
         result_pool = ctx.enter_context(tc.tile_pool(name="result_pool", bufs=16))
         psum = ctx.enter_context(tc.psum_pool(name="psum", bufs=1))
 
-        zeros = keep.tile([P, N_CHUNK], BF16)
-        nc.vector.memset(zeros[:], 0.0)
         w_planes = keep.tile([P, N], U8, align_bytes=SLOT_BYTES)
         nc.vector.memset(w_planes[:].bitcast(I32), 0)
+        zeros = keep.tile([P, N_CHUNK], BF16)
+        nc.vector.memset(zeros[:].bitcast(I32), 0)
         identity = keep.tile([P, P], F32)
         make_identity(nc, identity[:])
+        identity_bf16 = keep.tile([P, P], BF16)
+        nc.scalar.copy(out=identity_bf16[:], in_=identity[:])
 
-        x_tiles = [x_pool.tile([P, K], BF16, name="x_tile") for i in range(ROW_TILES)]
+        bias_runs = keep.tile([P, BIAS_RUN], BF16)
+        nc.sync.dma_start(out=bias_runs[:], in_=bias.rearrange("(q c) -> q c", c=BIAS_RUN))
+
+        head_x = {}
+        x_tiles = {}
         w_words = [
             [
                 keep.tile(
@@ -63,19 +74,26 @@ def tile_sparselinearrelu_kernel(tc, x, weight_words, weight_scales, bias, out):
             ]
             for j in range(CHUNKS)
         ]
-        bias_all = keep.tile([P, N], BF16)
+
+        def load_head_x(g):
+            for duo in range(HEAD_TILES // DUO):
+                slice_x = head_pool.tile([P, DUO, K_PASS], BF16, name="slice_x")
+                rows = slice(duo * DUO * P, (duo + 1) * DUO * P)
+                nc.sync.dma_start(
+                    out=slice_x[:],
+                    in_=x[rows, g * K_PASS : (g + 1) * K_PASS].rearrange("(i r) k -> r i k", r=P),
+                )
+                head_x[g, duo] = slice_x
 
         def load_x(i):
+            x_tiles[i] = x_pool.tile([P, K], BF16, name="x_tile")
             nc.sync.dma_start(out=x_tiles[i][:], in_=x[i * P : (i + 1) * P, :])
 
-        def load_w(j):
-            for g in range(PASSES):
-                pass_bytes = weight_words[g].rearrange("p n t -> p (n t)")[
-                    :, j * N_CHUNK * PACK : (j + 1) * N_CHUNK * PACK
-                ]
-                nc.sync.dma_start(
-                    out=w_words[j][g][:].bitcast(I32), in_=pass_bytes.bitcast(I32)
-                )
+        def load_w(j, g):
+            pass_bytes = weight_words[g].rearrange("p n t -> p (n t)")[
+                :, j * N_CHUNK * PACK : (j + 1) * N_CHUNK * PACK
+            ]
+            nc.sync.dma_start(out=w_words[j][g][:].bitcast(I32), in_=pass_bytes.bitcast(I32))
 
         def load_scales(first_column, end_column):
             for quadrant in range(QUADRANTS):
@@ -92,17 +110,20 @@ def tile_sparselinearrelu_kernel(tc, x, weight_words, weight_scales, bias, out):
                     ].bitcast(I32),
                 )
 
-        load_x(0)
-        load_x(1)
+        load_head_x(0)
         load_scales(0, N_CHUNK)
-        load_w(0)
-        for i in range(2, ROW_TILES):
-            load_x(i)
+        load_w(0, 0)
+        for g in range(1, PASSES):
+            load_head_x(g)
+            load_w(0, g)
         load_scales(N_CHUNK, N)
-        load_w(1)
-        nc.sync.dma_start(out=bias_all[:], in_=bias.partition_broadcast(P))
-        load_w(2)
-        load_w(3)
+        for g in range(PASSES):
+            load_w(1, g)
+        for i in range(HEAD_TILES, ROW_TILES):
+            load_x(i)
+        for j in (2, 3):
+            for g in range(PASSES):
+                load_w(j, g)
 
         x_codes = keep.tile(
             [P, X_CODES_PAD + ROW_TILES * PASSES * P], U32, align_bytes=SLOT_BYTES
@@ -113,45 +134,79 @@ def tile_sparselinearrelu_kernel(tc, x, weight_words, weight_scales, bias, out):
             first_code_word = X_CODES_PAD + (i * PASSES + g) * P
             return x_codes[:, first_code_word : first_code_word + P].bitcast(FP8X4)
 
-        sorted_tiles = {}
+        def quantise_unit(i, g, grouped_unit):
+            nc.vector.quantize_mx(
+                out=x_words_of(i, g),
+                scales=x_scales[:, i, g, 0:P],
+                in_=grouped_unit.rearrange("p r t -> p (r t)"),
+            )
+
+        sorted_words = {}
         transposed = {}
         grouped_tiles = {}
         sums = {}
 
-        def sort_x(i):
-            sorted_x = sorted_pool.tile([P, K], BF16, name="sorted_x")
+        def sort_head(g, duo):
+            sorted_x = sorted_pool.tile([P, DUO, PAIRS, P], F32, name="sorted_duo")
             nc.vector.tensor_copy(
-                out=sorted_x[:].bitcast(F32).rearrange(
-                    "r (g u p) -> r g u p", g=PASSES, u=PAIRS
+                out=sorted_x[:],
+                in_=head_x[g, duo][:].rearrange("r i k -> r (i k)").bitcast(F32).rearrange(
+                    "r (i p u) -> r i u p", i=DUO, u=PAIRS
                 ),
+            )
+            sorted_words[g, duo] = sorted_x
+
+        def transpose_head(g, duo, bank, strided=False):
+            xt = psum.tile([P, DUO, PAIRS, P], F32, name="bank%d" % bank)
+            if strided:
+                words = head_x[g, duo][:].rearrange("r i k -> r (i k)").bitcast(F32)
+            for i in range(DUO):
+                for u in range(PAIRS):
+                    if strided:
+                        source = words[:, i * PAIRS * P + u : (i + 1) * PAIRS * P : PAIRS]
+                    else:
+                        source = sorted_words[g, duo][:, i, u, :]
+                    nc.tensor.transpose(xt[:, i, u, :], source, identity[:])
+            transposed[g, duo] = xt
+
+        def copy_head(g, duo):
+            grouped = grouped_pool.tile([P, DUO, P, PACK], BF16, align_bytes=64, name="grouped_duo")
+            nc.scalar.copy(
+                out=grouped[:].bitcast(F32),
+                in_=transposed[g, duo][:].rearrange("p i u r -> p i r u"),
+            )
+            grouped_tiles[g, duo] = grouped
+
+        def quantise_head(g, duo):
+            for i in range(DUO):
+                quantise_unit(duo * DUO + i, g, grouped_tiles[g, duo][:, i, :, :])
+
+        def sort_x(i):
+            sorted_x = sorted_pool.tile([P, PASSES, PAIRS, P], F32, name="sorted_x")
+            nc.vector.tensor_copy(
+                out=sorted_x[:],
                 in_=x_tiles[i][:].bitcast(F32).rearrange(
                     "r (g p u) -> r g u p", g=PASSES, u=PAIRS
                 ),
             )
-            sorted_tiles[i] = sorted_x
+            sorted_words[i] = sorted_x
 
-        def transpose_x(i):
-            words = sorted_tiles[i][:].bitcast(F32)
+        def transpose_x(i, banks):
             transposed[i] = []
             for half in range(2):
-                xt = psum.tile(
-                    [P, 2, PAIRS, P], F32, name="bank%d" % ((2 * i + half) % T_BANKS)
-                )
-                for t in range(2 * PAIRS):
-                    first_word = (2 * PAIRS * half + t) * P
-                    nc.tensor.transpose(
-                        xt[:, t // PAIRS, t % PAIRS, :],
-                        words[:, first_word : first_word + P],
-                        identity[:],
-                    )
+                xt = psum.tile([P, 2, PAIRS, P], F32, name="bank%d" % banks[half])
+                for g in range(2):
+                    for u in range(PAIRS):
+                        nc.tensor.transpose(
+                            xt[:, g, u, :], sorted_words[i][:, 2 * half + g, u, :], identity[:]
+                        )
                 transposed[i].append(xt)
 
-        def copy_out(i, first_on_vector):
+        def copy_out(i):
             grouped = grouped_pool.tile([P, PASSES, P, PACK], BF16, align_bytes=64, name="grouped")
             grouped_words = grouped[:].bitcast(F32)
             for half in range(2):
-                copy = nc.vector.tensor_copy if (half == 0 and first_on_vector) else nc.scalar.copy
-                copy(
+                nc.scalar.copy(
                     out=grouped_words[:, 2 * half : 2 * half + 2, :, :],
                     in_=transposed[i][half][:].rearrange("p g u r -> p g r u"),
                 )
@@ -159,44 +214,51 @@ def tile_sparselinearrelu_kernel(tc, x, weight_words, weight_scales, bias, out):
 
         def quantise_x(i):
             for g in range(PASSES):
-                nc.vector.quantize_mx(
-                    out=x_words_of(i, g),
-                    scales=x_scales[:, i, g, 0:P],
-                    in_=grouped_tiles[i][:, g, :, :].rearrange("p r t -> p (r t)"),
-                )
+                quantise_unit(i, g, grouped_tiles[i][:, g, :, :])
 
-        def multiply(b, first=0, width=N_CHUNK, bank_shift=0):
-            j, i = b // ROW_TILES, b % ROW_TILES
-            columns = slice(j * N_CHUNK + first, j * N_CHUNK + first + width)
-            acc = psum.tile(
-                [P, width], F32, name="bank%d" % (((T_BANKS + b if b < T_BANKS else b) + bank_shift) % BANKS)
+        bias_all = keep.tile([P, N], F32, align_bytes=64)
+
+        def spread_bias(group, bank):
+            spread = psum.tile([P, BIAS_GROUP, P], F32, name="bank%d" % bank)
+            for c in range(BIAS_GROUP):
+                column = group * BIAS_GROUP + c
+                nc.tensor.matmul(
+                    out=spread[:, c, :],
+                    lhsT=bias_runs[:, column : column + 1].to_broadcast([P, P]),
+                    rhs=identity_bf16[:],
+                    start=True,
+                    stop=True,
+                )
+            nc.scalar.copy(
+                out=bias_all[:].rearrange("m (q c) -> m q c", c=BIAS_RUN)[
+                    :, :, group * BIAS_GROUP : (group + 1) * BIAS_GROUP
+                ],
+                in_=spread[:].rearrange("m c q -> m q c"),
             )
-            for g in range(PASSES):
-                nc.tensor.matmul_mx(
-                    out=acc[:],
-                    lhsT=x_words_of(i, g),
-                    lhsT_scale=x_scales[:, i, g, 0:P],
-                    rhs=w_words[j][g][:, first : first + width].bitcast(FP8X4),
-                    rhs_scale=w_planes[g * PLANE_ROWS : P, columns],
-                    start=(g == 0),
-                    stop=(g == PASSES - 1),
-                )
-            sums[b] = acc
 
-        def park(b):
-            parked = result_pool.tile([P, N_CHUNK], F32, name="result")
-            nc.scalar.copy(out=parked[:], in_=sums[b][:])
-            sums[b] = parked
-
-        def finish(b, first=0, width=N_CHUNK, parked=False):
-            j, i = b // ROW_TILES, b % ROW_TILES
+        def multiply_pass(acc, i, j, g, first=0, width=N_CHUNK):
             columns = slice(j * N_CHUNK + first, j * N_CHUNK + first + width)
-            if parked:
-                result = sums[b]
-            else:
-                result = result_pool.tile([P, width], F32, name="result")
+            nc.tensor.matmul_mx(
+                out=acc[:],
+                lhsT=x_words_of(i, g),
+                lhsT_scale=x_scales[:, i, g, 0:P],
+                rhs=w_words[j][g][:, first : first + width].bitcast(FP8X4),
+                rhs_scale=w_planes[g * PLANE_ROWS : P, columns],
+                start=(g == 0),
+                stop=(g == PASSES - 1),
+            )
+
+        def multiply(i, j, bank, first=0, width=N_CHUNK):
+            acc = psum.tile([P, width], F32, name="bank%d" % bank)
+            for g in range(PASSES):
+                multiply_pass(acc, i, j, g, first, width)
+            sums[i, j] = acc
+
+        def finish(i, j, first=0, width=N_CHUNK):
+            columns = slice(j * N_CHUNK + first, j * N_CHUNK + first + width)
+            result = result_pool.tile([P, width], F32, name="result")
             nc.vector.tensor_tensor(
-                out=result[:], in0=sums[b][:], in1=bias_all[:, columns], op=mybir.AluOpType.add
+                out=result[:], in0=sums[i, j][:], in1=bias_all[:, columns], op=mybir.AluOpType.add
             )
             nc.scalar.activation(
                 out=result[:], in_=result[:], func=mybir.ActivationFunctionType.Relu
@@ -211,62 +273,85 @@ def tile_sparselinearrelu_kernel(tc, x, weight_words, weight_scales, bias, out):
                     out=unread[:], lhsT=zeros[:, 0:P], rhs=zeros[:], start=True, stop=True
                 )
 
-        keep_clock_up(9)
-        for i in (0, 1):
-            sort_x(i)
-            transpose_x(i)
-            copy_out(i, False)
-            keep_clock_up(1)
-        quantise_x(0)
-        quantise_x(1)
-        multiply(0)
-        multiply(1)
-        park(0)
-        park(1)
-        keep_clock_up(1)
-        for i in (2, 3):
-            sort_x(i)
-            transpose_x(i)
-            copy_out(i, False)
-            keep_clock_up(1)
-        quantise_x(2)
+        duos = range(HEAD_TILES // DUO)
+        rotation = 0
+
+        keep_clock_up(5)
+        for duo in duos:
+            transpose_head(0, duo, rotation % T_BANKS, strided=True)
+            copy_head(0, duo)
+            rotation += 1
+        for group in (0, 1):
+            spread_bias(group, rotation % T_BANKS)
+            rotation += 1
+        accs = []
+        for g in range(PASSES):
+            if g + 1 < PASSES:
+                for duo in duos:
+                    sort_head(g + 1, duo)
+                for duo in duos:
+                    transpose_head(g + 1, duo, rotation % T_BANKS)
+                    copy_head(g + 1, duo)
+                    rotation += 1
+            for duo in duos:
+                quantise_head(g, duo)
+            for i in range(HEAD_TILES):
+                if g == 0:
+                    acc = psum.tile([P, N_CHUNK], F32, name="bank%d" % (T_BANKS + i))
+                    accs.append(acc)
+                multiply_pass(accs[i], i, 0, g)
+            if g < 2:
+                spread_bias(g + 2, rotation % T_BANKS)
+                rotation += 1
+        for i in range(HEAD_TILES):
+            sums[i, 0] = accs[i]
+
+        for i in range(HEAD_TILES):
+            finish(i, 0)
+        multiply(0, 1, 4)
+        finish(0, 1)
+        multiply(1, 1, 5)
         sort_x(4)
-        quantise_x(3)
+        multiply(2, 1, 6)
+        finish(1, 1)
+        transpose_x(4, (0, 1))
+        copy_out(4)
         sort_x(5)
-        multiply(2)
-        park(2)
-        transpose_x(4)
-        copy_out(4, False)
-        multiply(3)
-        park(3)
-        sort_x(6)
+        finish(2, 1)
+        multiply(3, 1, 7)
         quantise_x(4)
-        transpose_x(5)
-        copy_out(5, False)
-        multiply(4)
-        sort_x(7)
+        transpose_x(5, (2, 3))
+        copy_out(5)
+        finish(3, 1)
+        sort_x(6)
+        multiply(4, 0, 4)
         quantise_x(5)
-        transpose_x(6)
-        copy_out(6, False)
-        multiply(5)
+        transpose_x(6, (0, 1))
+        copy_out(6)
+        finish(4, 0)
+        multiply(4, 1, 5)
+        sort_x(7)
+        multiply(5, 0, 6)
         quantise_x(6)
-        transpose_x(7)
-        copy_out(7, False)
-        multiply(6)
+        finish(4, 1)
+        transpose_x(7, (2, 3))
+        copy_out(7)
+        finish(5, 0)
+        multiply(5, 1, 7)
         quantise_x(7)
-        multiply(ROW_TILES)
-        multiply(ROW_TILES + 1)
-        multiply(7)
-        for b in range(4, ROW_TILES):
-            finish(b)
-        for early in range(4):
-            finish(early, parked=True)
-        finish(ROW_TILES)
-        finish(ROW_TILES + 1)
-        last = ROW_TILES * CHUNKS - 1
-        for b in range(ROW_TILES + 2, last):
-            multiply(b)
-            finish(b)
+        finish(5, 1)
+        blocks = [(6, 0), (6, 1), (7, 0), (7, 1)]
+        for n, (i, j) in enumerate(blocks):
+            multiply(i, j, T_BANKS + n)
+            finish(i, j)
+        last = (ROW_TILES - 1, CHUNKS - 1)
+        bank = 0
+        for j in (2, 3):
+            for i in range(ROW_TILES):
+                if (i, j) != last:
+                    multiply(i, j, bank % BANKS)
+                    finish(i, j)
+                    bank += 1
         for half in range(2):
-            multiply(last, half * N_CHUNK // 2, N_CHUNK // 2, half)
-            finish(last, half * N_CHUNK // 2, N_CHUNK // 2)
+            multiply(*last, (bank + half) % BANKS, half * N_CHUNK // 2, N_CHUNK // 2)
+            finish(*last, half * N_CHUNK // 2, N_CHUNK // 2)

@@ -32,9 +32,12 @@ BANKS = 8
 T_BANKS = 4
 
 HEAD_TILES = 4
-DUO = 2
+HALVES = 2
+HALF_K = K // HALVES
+HALF_PASSES = PASSES // HALVES
 BIAS_RUN = N // P
-BIAS_GROUP = BIAS_RUN // PASSES
+BIAS_BANKS = 2
+BIAS_GROUP = BIAS_RUN // BIAS_BANKS
 
 FLOPS = 2 * ROWS * K * N
 
@@ -44,10 +47,9 @@ def tile_sparselinearrelu_kernel(tc, x, weight_words, weight_scales, bias, out):
     with ExitStack() as ctx:
         ctx.enter_context(tc.manual_schedule())
         keep = ctx.enter_context(tc.tile_pool(name="keep", bufs=1))
-        x_pool = ctx.enter_context(tc.tile_pool(name="x_pool", bufs=ROW_TILES - HEAD_TILES))
-        head_pool = ctx.enter_context(tc.tile_pool(name="head_pool", bufs=PASSES * HEAD_TILES // DUO))
-        sorted_pool = ctx.enter_context(tc.tile_pool(name="sorted_pool", bufs=4))
-        grouped_pool = ctx.enter_context(tc.tile_pool(name="grouped_pool", bufs=4))
+        x_pool = ctx.enter_context(tc.tile_pool(name="x_pool", bufs=ROW_TILES))
+        sorted_pool = ctx.enter_context(tc.tile_pool(name="sorted_pool", bufs=6))
+        grouped_pool = ctx.enter_context(tc.tile_pool(name="grouped_pool", bufs=6))
         result_pool = ctx.enter_context(tc.tile_pool(name="result_pool", bufs=16))
         psum = ctx.enter_context(tc.psum_pool(name="psum", bufs=1))
 
@@ -63,8 +65,7 @@ def tile_sparselinearrelu_kernel(tc, x, weight_words, weight_scales, bias, out):
         bias_runs = keep.tile([P, BIAS_RUN], BF16)
         nc.sync.dma_start(out=bias_runs[:], in_=bias.rearrange("(q c) -> q c", c=BIAS_RUN))
 
-        head_x = {}
-        x_tiles = {}
+        x_tiles = [x_pool.tile([P, K], BF16, name="x_tile") for i in range(ROW_TILES)]
         w_words = [
             [
                 keep.tile(
@@ -75,19 +76,10 @@ def tile_sparselinearrelu_kernel(tc, x, weight_words, weight_scales, bias, out):
             for j in range(CHUNKS)
         ]
 
-        def load_head_x(g):
-            for duo in range(HEAD_TILES // DUO):
-                slice_x = head_pool.tile([P, DUO, K_PASS], BF16, name="slice_x")
-                rows = slice(duo * DUO * P, (duo + 1) * DUO * P)
-                nc.sync.dma_start(
-                    out=slice_x[:],
-                    in_=x[rows, g * K_PASS : (g + 1) * K_PASS].rearrange("(i r) k -> r i k", r=P),
-                )
-                head_x[g, duo] = slice_x
-
-        def load_x(i):
-            x_tiles[i] = x_pool.tile([P, K], BF16, name="x_tile")
-            nc.sync.dma_start(out=x_tiles[i][:], in_=x[i * P : (i + 1) * P, :])
+        def load_x(i, first_k=0, end_k=K):
+            nc.sync.dma_start(
+                out=x_tiles[i][:, first_k:end_k], in_=x[i * P : (i + 1) * P, first_k:end_k]
+            )
 
         def load_w(j, g):
             pass_bytes = weight_words[g].rearrange("p n t -> p (n t)")[
@@ -110,17 +102,21 @@ def tile_sparselinearrelu_kernel(tc, x, weight_words, weight_scales, bias, out):
                     ].bitcast(I32),
                 )
 
-        load_head_x(0)
-        load_scales(0, N_CHUNK)
-        load_w(0, 0)
-        for g in range(1, PASSES):
-            load_head_x(g)
-            load_w(0, g)
-        load_scales(N_CHUNK, N)
-        for g in range(PASSES):
+        for h in range(HALVES):
+            for i in range(HEAD_TILES):
+                load_x(i, h * HALF_K, (h + 1) * HALF_K)
+            if h == 0:
+                load_scales(0, N_CHUNK)
+            for g in range(h * HALF_PASSES, (h + 1) * HALF_PASSES):
+                load_w(0, g)
+        load_scales(N_CHUNK, 2 * N_CHUNK)
+        for g in range(PASSES - 1):
             load_w(1, g)
-        for i in range(HEAD_TILES, ROW_TILES):
+        load_x(HEAD_TILES)
+        load_w(1, PASSES - 1)
+        for i in range(HEAD_TILES + 1, ROW_TILES):
             load_x(i)
+        load_scales(2 * N_CHUNK, N)
         for j in (2, 3):
             for g in range(PASSES):
                 load_w(j, g)
@@ -134,112 +130,79 @@ def tile_sparselinearrelu_kernel(tc, x, weight_words, weight_scales, bias, out):
             first_code_word = X_CODES_PAD + (i * PASSES + g) * P
             return x_codes[:, first_code_word : first_code_word + P].bitcast(FP8X4)
 
-        def quantise_unit(i, g, grouped_unit):
-            nc.vector.quantize_mx(
-                out=x_words_of(i, g),
-                scales=x_scales[:, i, g, 0:P],
-                in_=grouped_unit.rearrange("p r t -> p (r t)"),
-            )
-
-        sorted_words = {}
+        sorted_halves = {}
         transposed = {}
-        grouped_tiles = {}
+        grouped_halves = {}
         sums = {}
+        results = {}
 
-        def sort_head(g, duo):
-            sorted_x = sorted_pool.tile([P, DUO, PAIRS, P], F32, name="sorted_duo")
+        def sort_half(i, h):
+            sorted_x = sorted_pool.tile([P, HALF_PASSES, PAIRS, P], F32, name="sorted_x")
             nc.vector.tensor_copy(
                 out=sorted_x[:],
-                in_=head_x[g, duo][:].rearrange("r i k -> r (i k)").bitcast(F32).rearrange(
-                    "r (i p u) -> r i u p", i=DUO, u=PAIRS
+                in_=x_tiles[i][:, h * HALF_K : (h + 1) * HALF_K].bitcast(F32).rearrange(
+                    "r (g p u) -> r g u p", g=HALF_PASSES, u=PAIRS
                 ),
             )
-            sorted_words[g, duo] = sorted_x
+            sorted_halves[i, h] = sorted_x
 
-        def transpose_head(g, duo, bank, strided=False):
-            xt = psum.tile([P, DUO, PAIRS, P], F32, name="bank%d" % bank)
-            if strided:
-                words = head_x[g, duo][:].rearrange("r i k -> r (i k)").bitcast(F32)
-            for i in range(DUO):
+        def transpose_half(i, h, bank):
+            xt = psum.tile([P, HALF_PASSES, PAIRS, P], F32, name="bank%d" % bank)
+            for g in range(HALF_PASSES):
                 for u in range(PAIRS):
-                    if strided:
-                        source = words[:, i * PAIRS * P + u : (i + 1) * PAIRS * P : PAIRS]
-                    else:
-                        source = sorted_words[g, duo][:, i, u, :]
-                    nc.tensor.transpose(xt[:, i, u, :], source, identity[:])
-            transposed[g, duo] = xt
+                    nc.tensor.transpose(
+                        xt[:, g, u, :], sorted_halves[i, h][:, g, u, :], identity[:]
+                    )
+            transposed[i, h] = xt
 
-        def copy_head(g, duo):
-            grouped = grouped_pool.tile([P, DUO, P, PACK], BF16, align_bytes=64, name="grouped_duo")
+        def copy_half(i, h):
+            grouped = grouped_pool.tile(
+                [P, HALF_PASSES, P, PACK], BF16, align_bytes=64, name="grouped"
+            )
             nc.scalar.copy(
                 out=grouped[:].bitcast(F32),
-                in_=transposed[g, duo][:].rearrange("p i u r -> p i r u"),
+                in_=transposed[i, h][:].rearrange("p g u r -> p g r u"),
             )
-            grouped_tiles[g, duo] = grouped
+            grouped_halves[i, h] = grouped
 
-        def quantise_head(g, duo):
-            for i in range(DUO):
-                quantise_unit(duo * DUO + i, g, grouped_tiles[g, duo][:, i, :, :])
-
-        def sort_x(i):
-            sorted_x = sorted_pool.tile([P, PASSES, PAIRS, P], F32, name="sorted_x")
-            nc.vector.tensor_copy(
-                out=sorted_x[:],
-                in_=x_tiles[i][:].bitcast(F32).rearrange(
-                    "r (g p u) -> r g u p", g=PASSES, u=PAIRS
-                ),
-            )
-            sorted_words[i] = sorted_x
-
-        def transpose_x(i, banks):
-            transposed[i] = []
-            for half in range(2):
-                xt = psum.tile([P, 2, PAIRS, P], F32, name="bank%d" % banks[half])
-                for g in range(2):
-                    for u in range(PAIRS):
-                        nc.tensor.transpose(
-                            xt[:, g, u, :], sorted_words[i][:, 2 * half + g, u, :], identity[:]
-                        )
-                transposed[i].append(xt)
-
-        def copy_out(i):
-            grouped = grouped_pool.tile([P, PASSES, P, PACK], BF16, align_bytes=64, name="grouped")
-            grouped_words = grouped[:].bitcast(F32)
-            for half in range(2):
-                nc.scalar.copy(
-                    out=grouped_words[:, 2 * half : 2 * half + 2, :, :],
-                    in_=transposed[i][half][:].rearrange("p g u r -> p g r u"),
+        def quantise_half(i, h):
+            for g in range(HALF_PASSES):
+                nc.vector.quantize_mx(
+                    out=x_words_of(i, h * HALF_PASSES + g),
+                    scales=x_scales[:, i, h * HALF_PASSES + g, 0:P],
+                    in_=grouped_halves[i, h][:, g, :, :].rearrange("p r t -> p (r t)"),
                 )
-            grouped_tiles[i] = grouped
 
-        def quantise_x(i):
-            for g in range(PASSES):
-                quantise_unit(i, g, grouped_tiles[i][:, g, :, :])
-
-        bias_all = keep.tile([P, N], F32, align_bytes=64)
+        bias_all = keep.tile([P, N], BF16, align_bytes=64)
+        spread = {}
 
         def spread_bias(group, bank):
-            spread = psum.tile([P, BIAS_GROUP, P], F32, name="bank%d" % bank)
+            spread[group] = psum.tile([P, BIAS_GROUP, P], BF16, name="bank%d" % bank)
             for c in range(BIAS_GROUP):
                 column = group * BIAS_GROUP + c
                 nc.tensor.matmul(
-                    out=spread[:, c, :],
+                    out=spread[group][:, c, :],
                     lhsT=bias_runs[:, column : column + 1].to_broadcast([P, P]),
                     rhs=identity_bf16[:],
                     start=True,
                     stop=True,
                 )
+
+        def copy_bias(group):
             nc.scalar.copy(
                 out=bias_all[:].rearrange("m (q c) -> m q c", c=BIAS_RUN)[
                     :, :, group * BIAS_GROUP : (group + 1) * BIAS_GROUP
                 ],
-                in_=spread[:].rearrange("m c q -> m q c"),
+                in_=spread[group][:].rearrange("m c q -> m q c"),
             )
 
-        def multiply_pass(acc, i, j, g, first=0, width=N_CHUNK):
+        def open_block(i, j, bank, width=N_CHUNK):
+            sums[i, j] = psum.tile([P, width], F32, name="bank%d" % bank)
+
+        def multiply_pass(i, j, g, first=0, width=N_CHUNK):
             columns = slice(j * N_CHUNK + first, j * N_CHUNK + first + width)
             nc.tensor.matmul_mx(
-                out=acc[:],
+                out=sums[i, j][:],
                 lhsT=x_words_of(i, g),
                 lhsT_scale=x_scales[:, i, g, 0:P],
                 rhs=w_words[j][g][:, first : first + width].bitcast(FP8X4),
@@ -249,109 +212,143 @@ def tile_sparselinearrelu_kernel(tc, x, weight_words, weight_scales, bias, out):
             )
 
         def multiply(i, j, bank, first=0, width=N_CHUNK):
-            acc = psum.tile([P, width], F32, name="bank%d" % bank)
+            open_block(i, j, bank, width)
             for g in range(PASSES):
-                multiply_pass(acc, i, j, g, first, width)
-            sums[i, j] = acc
+                multiply_pass(i, j, g, first, width)
+
+        def add_bias(i, j, first=0, width=N_CHUNK):
+            columns = slice(j * N_CHUNK + first, j * N_CHUNK + first + width)
+            results[i, j] = result_pool.tile([P, width], F32, name="result")
+            nc.vector.tensor_tensor(
+                out=results[i, j][:], in0=sums[i, j][:], in1=bias_all[:, columns],
+                op=mybir.AluOpType.add,
+            )
+
+        def relu_and_store(i, j, first=0, width=N_CHUNK):
+            columns = slice(j * N_CHUNK + first, j * N_CHUNK + first + width)
+            nc.scalar.activation(
+                out=results[i, j][:], in_=results[i, j][:],
+                func=mybir.ActivationFunctionType.Relu,
+            )
+            nc.sync.dma_start(out=out[i * P : (i + 1) * P, columns], in_=results[i, j][:])
 
         def finish(i, j, first=0, width=N_CHUNK):
-            columns = slice(j * N_CHUNK + first, j * N_CHUNK + first + width)
-            result = result_pool.tile([P, width], F32, name="result")
-            nc.vector.tensor_tensor(
-                out=result[:], in0=sums[i, j][:], in1=bias_all[:, columns], op=mybir.AluOpType.add
-            )
-            nc.scalar.activation(
-                out=result[:], in_=result[:], func=mybir.ActivationFunctionType.Relu
-            )
-            nc.sync.dma_start(out=out[i * P : (i + 1) * P, columns], in_=result[:])
+            add_bias(i, j, first, width)
+            relu_and_store(i, j, first, width)
 
-        unread = psum.tile([P, N_CHUNK], F32, name="bank%d" % (BANKS - 1))
-
-        def keep_clock_up(count):
+        def keep_clock_up_in(bank, count):
+            unread = psum.tile([P, N_CHUNK], F32, name="bank%d" % bank)
             for repeat in range(count):
                 nc.tensor.matmul(
                     out=unread[:], lhsT=zeros[:, 0:P], rhs=zeros[:], start=True, stop=True
                 )
 
-        duos = range(HEAD_TILES // DUO)
-        rotation = 0
+        def keep_clock_up(count):
+            keep_clock_up_in(4, count)
 
-        keep_clock_up(5)
-        for duo in duos:
-            transpose_head(0, duo, rotation % T_BANKS, strided=True)
-            copy_head(0, duo)
-            rotation += 1
-        for group in (0, 1):
-            spread_bias(group, rotation % T_BANKS)
-            rotation += 1
-        accs = []
-        for g in range(PASSES):
-            if g + 1 < PASSES:
-                for duo in duos:
-                    sort_head(g + 1, duo)
-                for duo in duos:
-                    transpose_head(g + 1, duo, rotation % T_BANKS)
-                    copy_head(g + 1, duo)
-                    rotation += 1
-            for duo in duos:
-                quantise_head(g, duo)
-            for i in range(HEAD_TILES):
-                if g == 0:
-                    acc = psum.tile([P, N_CHUNK], F32, name="bank%d" % (T_BANKS + i))
-                    accs.append(acc)
-                multiply_pass(accs[i], i, 0, g)
-            if g < 2:
-                spread_bias(g + 2, rotation % T_BANKS)
-                rotation += 1
-        for i in range(HEAD_TILES):
-            sums[i, 0] = accs[i]
+        head = range(HEAD_TILES)
 
-        for i in range(HEAD_TILES):
+        def multiply_half(i, j, h):
+            for g in range(h * HALF_PASSES, (h + 1) * HALF_PASSES):
+                multiply_pass(i, j, g)
+
+        keep_clock_up(4)
+        for i in (0, 1):
+            sort_half(i, 0)
+            transpose_half(i, 0, i)
+            copy_half(i, 0)
+            spread_bias(i, 6 + i)
+        copy_bias(0)
+        sort_half(2, 0)
+        quantise_half(0, 0)
+        transpose_half(2, 0, 2)
+        copy_half(2, 0)
+        keep_clock_up_in(4, 1)
+        sort_half(3, 0)
+        quantise_half(1, 0)
+        transpose_half(3, 0, 3)
+        copy_half(3, 0)
+        copy_bias(1)
+        quantise_half(2, 0)
+        quantise_half(3, 0)
+        for i in head:
+            open_block(i, 0, T_BANKS + i)
+        for i in (0, 1, 2):
+            multiply_half(i, 0, 0)
+        for i in head:
+            sort_half(i, 1)
+        for i in head:
+            transpose_half(i, 1, i)
+            copy_half(i, 1)
+            quantise_half(i, 1)
+            if i == 0:
+                multiply_half(3, 0, 0)
+        for i in head:
+            multiply_half(i, 0, 1)
+
+        for i in head:
             finish(i, 0)
-        multiply(0, 1, 4)
-        finish(0, 1)
-        multiply(1, 1, 5)
+            open_block(i, 1, (0, 1, 4, 5)[i])
+        for i in head:
+            multiply_half(i, 1, 0)
+        for i in head:
+            multiply_pass(i, 1, 2)
+
+        def turn(i, banks):
+            for h in range(HALVES):
+                transpose_half(i, h, banks[h])
+            for h in range(HALVES):
+                copy_half(i, h)
+
+        def sort_x(i):
+            for h in range(HALVES):
+                sort_half(i, h)
+
+        def quantise_x(i):
+            for h in range(HALVES):
+                quantise_half(i, h)
+
         sort_x(4)
-        multiply(2, 1, 6)
-        finish(1, 1)
-        transpose_x(4, (0, 1))
-        copy_out(4)
+        turn(4, (2, 3))
+        for i in head:
+            multiply_pass(i, 1, PASSES - 1)
         sort_x(5)
-        finish(2, 1)
-        multiply(3, 1, 7)
+        turn(5, (6, 7))
         quantise_x(4)
-        transpose_x(5, (2, 3))
-        copy_out(5)
-        finish(3, 1)
         sort_x(6)
-        multiply(4, 0, 4)
+        multiply(4, 0, 2)
+        finish(0, 1)
+        finish(1, 1)
+        multiply(4, 1, 3)
         quantise_x(5)
-        transpose_x(6, (0, 1))
-        copy_out(6)
+        turn(6, (0, 1))
+        finish(2, 1)
+        finish(3, 1)
         finish(4, 0)
-        multiply(4, 1, 5)
-        sort_x(7)
         multiply(5, 0, 6)
-        quantise_x(6)
-        finish(4, 1)
-        transpose_x(7, (2, 3))
-        copy_out(7)
-        finish(5, 0)
+        sort_x(7)
         multiply(5, 1, 7)
+        quantise_x(6)
+        turn(7, (4, 5))
+        finish(4, 1)
+        multiply(6, 0, 0)
+        finish(5, 0)
         quantise_x(7)
         finish(5, 1)
-        blocks = [(6, 0), (6, 1), (7, 0), (7, 1)]
-        for n, (i, j) in enumerate(blocks):
-            multiply(i, j, T_BANKS + n)
-            finish(i, j)
+        multiply(6, 1, 1)
+        finish(6, 0)
+        multiply(7, 0, 4)
+        finish(6, 1)
+        multiply(7, 1, 5)
+        finish(7, 0)
+        finish(7, 1)
+        banks = (2, 3, 6, 7, 0, 1, 4, 5)
         last = (ROW_TILES - 1, CHUNKS - 1)
-        bank = 0
-        for j in (2, 3):
-            for i in range(ROW_TILES):
-                if (i, j) != last:
-                    multiply(i, j, bank % BANKS)
-                    finish(i, j)
-                    bank += 1
+        turns = [(i, j) for j in (2, 3) for i in range(ROW_TILES) if (i, j) != last]
+        for n, (i, j) in enumerate(turns):
+            multiply(i, j, banks[n % BANKS])
+            finish(i, j)
         for half in range(2):
-            multiply(*last, (bank + half) % BANKS, half * N_CHUNK // 2, N_CHUNK // 2)
-            finish(*last, half * N_CHUNK // 2, N_CHUNK // 2)
+            first = half * N_CHUNK // 2
+            multiply(*last, banks[(len(turns) + half) % BANKS], first, N_CHUNK // 2)
+            finish(*last, first, N_CHUNK // 2)

@@ -48,7 +48,7 @@ def tile_sparselinearrelu_kernel(tc, x, weight_words, weight_scales, bias, out):
         ctx.enter_context(tc.manual_schedule())
         keep = ctx.enter_context(tc.tile_pool(name="keep", bufs=1))
         x_pool = ctx.enter_context(tc.tile_pool(name="x_pool", bufs=ROW_TILES))
-        sorted_pool = ctx.enter_context(tc.tile_pool(name="sorted_pool", bufs=6))
+        sorted_pool = ctx.enter_context(tc.tile_pool(name="sorted_pool", bufs=8))
         grouped_pool = ctx.enter_context(tc.tile_pool(name="grouped_pool", bufs=6))
         result_pool = ctx.enter_context(tc.tile_pool(name="result_pool", bufs=16))
         psum = ctx.enter_context(tc.psum_pool(name="psum", bufs=1))
@@ -148,18 +148,21 @@ def tile_sparselinearrelu_kernel(tc, x, weight_words, weight_scales, bias, out):
 
         def transpose_half(i, h, bank):
             xt = psum.tile([P, HALF_PASSES, PAIRS, P], F32, name="bank%d" % bank)
+            words = x_tiles[i][:, h * HALF_K : (h + 1) * HALF_K].bitcast(F32)
             for g in range(HALF_PASSES):
                 for u in range(PAIRS):
-                    nc.tensor.transpose(
-                        xt[:, g, u, :], sorted_halves[i, h][:, g, u, :], identity[:]
-                    )
+                    if (i, h) in sorted_halves:
+                        source = sorted_halves[i, h][:, g, u, :]
+                    else:
+                        source = words[:, PAIRS * P * g + u : PAIRS * P * (g + 1) : PAIRS]
+                    nc.tensor.transpose(xt[:, g, u, :], source, identity[:])
             transposed[i, h] = xt
 
-        def copy_half(i, h):
+        def copy_half(i, h, copy=nc.scalar.copy):
             grouped = grouped_pool.tile(
                 [P, HALF_PASSES, P, PACK], BF16, align_bytes=64, name="grouped"
             )
-            nc.scalar.copy(
+            copy(
                 out=grouped[:].bitcast(F32),
                 in_=transposed[i, h][:].rearrange("p g u r -> p g r u"),
             )
@@ -189,7 +192,7 @@ def tile_sparselinearrelu_kernel(tc, x, weight_words, weight_scales, bias, out):
                 )
 
         def copy_bias(group):
-            nc.scalar.copy(
+            nc.vector.tensor_copy(
                 out=bias_all[:].rearrange("m (q c) -> m q c", c=BIAS_RUN)[
                     :, :, group * BIAS_GROUP : (group + 1) * BIAS_GROUP
                 ],
@@ -252,37 +255,34 @@ def tile_sparselinearrelu_kernel(tc, x, weight_words, weight_scales, bias, out):
             for g in range(h * HALF_PASSES, (h + 1) * HALF_PASSES):
                 multiply_pass(i, j, g)
 
-        keep_clock_up(4)
-        for i in (0, 1):
-            sort_half(i, 0)
+        keep_clock_up(2)
+        spread_bias(0, 6)
+        copy_bias(0)
+        for i in head:
             transpose_half(i, 0, i)
             copy_half(i, 0)
-            spread_bias(i, 6 + i)
-        copy_bias(0)
-        sort_half(2, 0)
-        quantise_half(0, 0)
-        transpose_half(2, 0, 2)
-        copy_half(2, 0)
-        keep_clock_up_in(4, 1)
-        sort_half(3, 0)
-        quantise_half(1, 0)
-        transpose_half(3, 0, 3)
-        copy_half(3, 0)
-        copy_bias(1)
-        quantise_half(2, 0)
-        quantise_half(3, 0)
+            quantise_half(i, 0)
+            if i == 1:
+                spread_bias(1, 7)
+                copy_bias(1)
         for i in head:
             open_block(i, 0, T_BANKS + i)
-        for i in (0, 1, 2):
-            multiply_half(i, 0, 0)
-        for i in head:
-            sort_half(i, 1)
-        for i in head:
+        for g in range(HALF_PASSES):
+            for i in (0, 1):
+                multiply_pass(i, 0, g)
+        for i in (0, 1):
+            transpose_half(i, 1, i)
+            copy_half(i, 1)
+        multiply_half(2, 0, 0)
+        multiply_half(3, 0, 0)
+        sort_half(2, 1)
+        sort_half(3, 1)
+        quantise_half(0, 1)
+        quantise_half(1, 1)
+        for i in (2, 3):
             transpose_half(i, 1, i)
             copy_half(i, 1)
             quantise_half(i, 1)
-            if i == 0:
-                multiply_half(3, 0, 0)
         for i in head:
             multiply_half(i, 0, 1)
 
@@ -308,31 +308,29 @@ def tile_sparselinearrelu_kernel(tc, x, weight_words, weight_scales, bias, out):
             for h in range(HALVES):
                 quantise_half(i, h)
 
-        sort_x(4)
+        for i in (4, 5, 6, 7):
+            sort_x(i)
         turn(4, (2, 3))
+        turn(5, (6, 7))
         for i in head:
             multiply_pass(i, 1, PASSES - 1)
-        sort_x(5)
-        turn(5, (6, 7))
         quantise_x(4)
-        sort_x(6)
         multiply(4, 0, 2)
         finish(0, 1)
         finish(1, 1)
         multiply(4, 1, 3)
         quantise_x(5)
-        turn(6, (0, 1))
         finish(2, 1)
         finish(3, 1)
-        finish(4, 0)
         multiply(5, 0, 6)
-        sort_x(7)
+        turn(6, (0, 1))
+        turn(7, (4, 5))
+        finish(4, 0)
+        finish(4, 1)
         multiply(5, 1, 7)
         quantise_x(6)
-        turn(7, (4, 5))
-        finish(4, 1)
-        multiply(6, 0, 0)
         finish(5, 0)
+        multiply(6, 0, 0)
         quantise_x(7)
         finish(5, 1)
         multiply(6, 1, 1)

@@ -35,9 +35,6 @@ HEAD_TILES = 4
 HALVES = 2
 HALF_K = K // HALVES
 HALF_PASSES = PASSES // HALVES
-BIAS_RUN = N // P
-BIAS_BANKS = 2
-BIAS_GROUP = BIAS_RUN // BIAS_BANKS
 
 FLOPS = 2 * ROWS * K * N
 
@@ -59,11 +56,6 @@ def tile_sparselinearrelu_kernel(tc, x, weight_words, weight_scales, bias, out):
         nc.vector.memset(zeros[:].bitcast(I32), 0)
         identity = keep.tile([P, P], F32)
         make_identity(nc, identity[:])
-        identity_bf16 = keep.tile([P, P], BF16)
-        nc.scalar.copy(out=identity_bf16[:], in_=identity[:])
-
-        bias_runs = keep.tile([P, BIAS_RUN], BF16)
-        nc.sync.dma_start(out=bias_runs[:], in_=bias.rearrange("(q c) -> q c", c=BIAS_RUN))
 
         x_tiles = [x_pool.tile([P, K], BF16, name="x_tile") for i in range(ROW_TILES)]
         w_words = [
@@ -109,6 +101,8 @@ def tile_sparselinearrelu_kernel(tc, x, weight_words, weight_scales, bias, out):
                 load_scales(0, N_CHUNK)
             for g in range(h * HALF_PASSES, (h + 1) * HALF_PASSES):
                 load_w(0, g)
+        bias_all = keep.tile([P, N], BF16)
+        nc.sync.dma_start(out=bias_all[:], in_=bias.partition_broadcast(P))
         load_scales(N_CHUNK, 2 * N_CHUNK)
         for g in range(PASSES - 1):
             load_w(1, g)
@@ -124,11 +118,15 @@ def tile_sparselinearrelu_kernel(tc, x, weight_words, weight_scales, bias, out):
         x_codes = keep.tile(
             [P, X_CODES_PAD + ROW_TILES * PASSES * P], U32, align_bytes=SLOT_BYTES
         )
-        x_scales = keep.tile([P, ROW_TILES, PASSES, SLOT_BYTES], U8, align_bytes=SLOT_BYTES)
+        x_scales = keep.tile([P, ROW_TILES * PASSES * P], U8, align_bytes=SLOT_BYTES)
 
-        def x_words_of(i, g):
+        def x_words_of(i, g, passes=1):
             first_code_word = X_CODES_PAD + (i * PASSES + g) * P
-            return x_codes[:, first_code_word : first_code_word + P].bitcast(FP8X4)
+            return x_codes[:, first_code_word : first_code_word + passes * P].bitcast(FP8X4)
+
+        def x_scales_of(i, g, passes=1):
+            first_byte = (i * PASSES + g) * P
+            return x_scales[:, first_byte : first_byte + passes * P]
 
         sorted_halves = {}
         transposed = {}
@@ -169,34 +167,10 @@ def tile_sparselinearrelu_kernel(tc, x, weight_words, weight_scales, bias, out):
             grouped_halves[i, h] = grouped
 
         def quantise_half(i, h):
-            for g in range(HALF_PASSES):
-                nc.vector.quantize_mx(
-                    out=x_words_of(i, h * HALF_PASSES + g),
-                    scales=x_scales[:, i, h * HALF_PASSES + g, 0:P],
-                    in_=grouped_halves[i, h][:, g, :, :].rearrange("p r t -> p (r t)"),
-                )
-
-        bias_all = keep.tile([P, N], BF16, align_bytes=64)
-        spread = {}
-
-        def spread_bias(group, bank):
-            spread[group] = psum.tile([P, BIAS_GROUP, P], BF16, name="bank%d" % bank)
-            for c in range(BIAS_GROUP):
-                column = group * BIAS_GROUP + c
-                nc.tensor.matmul(
-                    out=spread[group][:, c, :],
-                    lhsT=bias_runs[:, column : column + 1].to_broadcast([P, P]),
-                    rhs=identity_bf16[:],
-                    start=True,
-                    stop=True,
-                )
-
-        def copy_bias(group):
-            nc.vector.tensor_copy(
-                out=bias_all[:].rearrange("m (q c) -> m q c", c=BIAS_RUN)[
-                    :, :, group * BIAS_GROUP : (group + 1) * BIAS_GROUP
-                ],
-                in_=spread[group][:].rearrange("m c q -> m q c"),
+            nc.vector.quantize_mx(
+                out=x_words_of(i, h * HALF_PASSES, HALF_PASSES),
+                scales=x_scales_of(i, h * HALF_PASSES, HALF_PASSES),
+                in_=grouped_halves[i, h][:].rearrange("p g r t -> p (g r t)"),
             )
 
         def open_block(i, j, bank, width=N_CHUNK):
@@ -207,7 +181,7 @@ def tile_sparselinearrelu_kernel(tc, x, weight_words, weight_scales, bias, out):
             nc.tensor.matmul_mx(
                 out=sums[i, j][:],
                 lhsT=x_words_of(i, g),
-                lhsT_scale=x_scales[:, i, g, 0:P],
+                lhsT_scale=x_scales_of(i, g),
                 rhs=w_words[j][g][:, first : first + width].bitcast(FP8X4),
                 rhs_scale=w_planes[g * PLANE_ROWS : P, columns],
                 start=(g == 0),
@@ -255,32 +229,32 @@ def tile_sparselinearrelu_kernel(tc, x, weight_words, weight_scales, bias, out):
             for g in range(h * HALF_PASSES, (h + 1) * HALF_PASSES):
                 multiply_pass(i, j, g)
 
-        keep_clock_up(2)
-        spread_bias(0, 6)
-        copy_bias(0)
+        keep_clock_up(5)
+        for i in head:
+            sort_half(i, 0)
         for i in head:
             transpose_half(i, 0, i)
             copy_half(i, 0)
-            quantise_half(i, 0)
-            if i == 1:
-                spread_bias(1, 7)
-                copy_bias(1)
         for i in head:
             open_block(i, 0, T_BANKS + i)
+        quantise_half(0, 0)
+        quantise_half(1, 0)
+        sort_half(0, 1)
+        quantise_half(2, 0)
+        sort_half(1, 1)
+        quantise_half(3, 0)
+        sort_half(2, 1)
+        sort_half(3, 1)
         for g in range(HALF_PASSES):
             for i in (0, 1):
                 multiply_pass(i, 0, g)
-        for i in (0, 1):
-            transpose_half(i, 1, i)
-            copy_half(i, 1)
+        transpose_half(0, 1, 0)
+        transpose_half(1, 1, 1)
         multiply_half(2, 0, 0)
         multiply_half(3, 0, 0)
-        sort_half(2, 1)
-        sort_half(3, 1)
-        quantise_half(0, 1)
-        quantise_half(1, 1)
-        for i in (2, 3):
-            transpose_half(i, 1, i)
+        transpose_half(2, 1, 2)
+        transpose_half(3, 1, 3)
+        for i in head:
             copy_half(i, 1)
             quantise_half(i, 1)
         for i in head:

@@ -35,6 +35,9 @@ HEAD_TILES = 4
 HALVES = 2
 HALF_K = K // HALVES
 HALF_PASSES = PASSES // HALVES
+BIAS_RUN = N // P
+BIAS_BANKS = 2
+BIAS_GROUP = BIAS_RUN // BIAS_BANKS
 
 FLOPS = 2 * ROWS * K * N
 
@@ -56,6 +59,11 @@ def tile_sparselinearrelu_kernel(tc, x, weight_words, weight_scales, bias, out):
         nc.vector.memset(zeros[:].bitcast(I32), 0)
         identity = keep.tile([P, P], F32)
         make_identity(nc, identity[:])
+        identity_bf16 = keep.tile([P, P], BF16)
+        nc.scalar.copy(out=identity_bf16[:], in_=identity[:])
+
+        bias_runs = keep.tile([P, BIAS_RUN], BF16)
+        nc.sync.dma_start(out=bias_runs[:], in_=bias.rearrange("(q c) -> q c", c=BIAS_RUN))
 
         x_tiles = [x_pool.tile([P, K], BF16, name="x_tile") for i in range(ROW_TILES)]
         w_words = [
@@ -101,8 +109,6 @@ def tile_sparselinearrelu_kernel(tc, x, weight_words, weight_scales, bias, out):
                 load_scales(0, N_CHUNK)
             for g in range(h * HALF_PASSES, (h + 1) * HALF_PASSES):
                 load_w(0, g)
-        bias_all = keep.tile([P, N], BF16)
-        nc.sync.dma_start(out=bias_all[:], in_=bias.partition_broadcast(P))
         load_scales(N_CHUNK, 2 * N_CHUNK)
         for g in range(PASSES - 1):
             load_w(1, g)
@@ -173,6 +179,29 @@ def tile_sparselinearrelu_kernel(tc, x, weight_words, weight_scales, bias, out):
                 in_=grouped_halves[i, h][:].rearrange("p g r t -> p (g r t)"),
             )
 
+        bias_all = keep.tile([P, N], BF16, align_bytes=64)
+        spread = {}
+
+        def spread_bias(group, bank):
+            spread[group] = psum.tile([P, BIAS_GROUP, P], BF16, name="bank%d" % bank)
+            for c in range(BIAS_GROUP):
+                column = group * BIAS_GROUP + c
+                nc.tensor.matmul(
+                    out=spread[group][:, c, :],
+                    lhsT=bias_runs[:, column : column + 1].to_broadcast([P, P]),
+                    rhs=identity_bf16[:],
+                    start=True,
+                    stop=True,
+                )
+
+        def copy_bias(group):
+            nc.scalar.copy(
+                out=bias_all[:].rearrange("m (q c) -> m q c", c=BIAS_RUN)[
+                    :, :, group * BIAS_GROUP : (group + 1) * BIAS_GROUP
+                ],
+                in_=spread[group][:].rearrange("m c q -> m q c"),
+            )
+
         def open_block(i, j, bank, width=N_CHUNK):
             sums[i, j] = psum.tile([P, width], F32, name="bank%d" % bank)
 
@@ -229,7 +258,11 @@ def tile_sparselinearrelu_kernel(tc, x, weight_words, weight_scales, bias, out):
             for g in range(h * HALF_PASSES, (h + 1) * HALF_PASSES):
                 multiply_pass(i, j, g)
 
-        keep_clock_up(5)
+        keep_clock_up(2)
+        spread_bias(0, 6)
+        copy_bias(0)
+        spread_bias(1, 7)
+        copy_bias(1)
         for i in head:
             sort_half(i, 0)
         for i in head:
@@ -239,18 +272,18 @@ def tile_sparselinearrelu_kernel(tc, x, weight_words, weight_scales, bias, out):
             open_block(i, 0, T_BANKS + i)
         quantise_half(0, 0)
         quantise_half(1, 0)
-        sort_half(0, 1)
         quantise_half(2, 0)
-        sort_half(1, 1)
         quantise_half(3, 0)
+        sort_half(0, 1)
+        sort_half(1, 1)
         sort_half(2, 1)
         sort_half(3, 1)
         for g in range(HALF_PASSES):
             for i in (0, 1):
                 multiply_pass(i, 0, g)
+        multiply_half(2, 0, 0)
         transpose_half(0, 1, 0)
         transpose_half(1, 1, 1)
-        multiply_half(2, 0, 0)
         multiply_half(3, 0, 0)
         transpose_half(2, 1, 2)
         transpose_half(3, 1, 3)
@@ -282,8 +315,8 @@ def tile_sparselinearrelu_kernel(tc, x, weight_words, weight_scales, bias, out):
             for h in range(HALVES):
                 quantise_half(i, h)
 
-        for i in (4, 5, 6, 7):
-            sort_x(i)
+        sort_x(4)
+        sort_x(5)
         turn(4, (2, 3))
         turn(5, (6, 7))
         for i in head:
@@ -291,11 +324,13 @@ def tile_sparselinearrelu_kernel(tc, x, weight_words, weight_scales, bias, out):
         quantise_x(4)
         multiply(4, 0, 2)
         finish(0, 1)
+        sort_x(6)
         finish(1, 1)
         multiply(4, 1, 3)
         quantise_x(5)
         finish(2, 1)
         finish(3, 1)
+        sort_x(7)
         multiply(5, 0, 6)
         turn(6, (0, 1))
         turn(7, (4, 5))

@@ -35,9 +35,8 @@ HEAD_TILES = 4
 HALVES = 2
 HALF_K = K // HALVES
 HALF_PASSES = PASSES // HALVES
-BIAS_RUN = N // P
 BIAS_BANKS = 2
-BIAS_GROUP = BIAS_RUN // BIAS_BANKS
+BIAS_GROUP = CHUNKS // BIAS_BANKS
 
 FLOPS = 2 * ROWS * K * N
 
@@ -57,13 +56,17 @@ def tile_sparselinearrelu_kernel(tc, x, weight_words, weight_scales, bias, out):
         nc.vector.memset(w_planes[:].bitcast(I32), 0)
         zeros = keep.tile([P, N_CHUNK], BF16)
         nc.vector.memset(zeros[:].bitcast(I32), 0)
+        bias_rows = keep.tile([P, N_CHUNK], BF16)
+        nc.gpsimd.memset(bias_rows[:], 0.0)
         identity = keep.tile([P, P], F32)
         make_identity(nc, identity[:])
         identity_bf16 = keep.tile([P, P], BF16)
         nc.scalar.copy(out=identity_bf16[:], in_=identity[:])
 
-        bias_runs = keep.tile([P, BIAS_RUN], BF16)
-        nc.sync.dma_start(out=bias_runs[:], in_=bias.rearrange("(q c) -> q c", c=BIAS_RUN))
+        def load_bias():
+            nc.sync.dma_start(
+                out=bias_rows[0:CHUNKS, :], in_=bias.rearrange("(j n) -> j n", n=N_CHUNK)
+            )
 
         x_tiles = [x_pool.tile([P, K], BF16, name="x_tile") for i in range(ROW_TILES)]
         w_words = [
@@ -105,6 +108,8 @@ def tile_sparselinearrelu_kernel(tc, x, weight_words, weight_scales, bias, out):
         for h in range(HALVES):
             for i in range(HEAD_TILES):
                 load_x(i, h * HALF_K, (h + 1) * HALF_K)
+                if (i, h) == (1, 0):
+                    load_bias()
             if h == 0:
                 load_scales(0, N_CHUNK)
             for g in range(h * HALF_PASSES, (h + 1) * HALF_PASSES):
@@ -124,15 +129,11 @@ def tile_sparselinearrelu_kernel(tc, x, weight_words, weight_scales, bias, out):
         x_codes = keep.tile(
             [P, X_CODES_PAD + ROW_TILES * PASSES * P], U32, align_bytes=SLOT_BYTES
         )
-        x_scales = keep.tile([P, ROW_TILES * PASSES * P], U8, align_bytes=SLOT_BYTES)
+        x_scales = keep.tile([P, ROW_TILES, PASSES, SLOT_BYTES], U8, align_bytes=SLOT_BYTES)
 
-        def x_words_of(i, g, passes=1):
+        def x_words_of(i, g):
             first_code_word = X_CODES_PAD + (i * PASSES + g) * P
-            return x_codes[:, first_code_word : first_code_word + passes * P].bitcast(FP8X4)
-
-        def x_scales_of(i, g, passes=1):
-            first_byte = (i * PASSES + g) * P
-            return x_scales[:, first_byte : first_byte + passes * P]
+            return x_codes[:, first_code_word : first_code_word + P].bitcast(FP8X4)
 
         sorted_halves = {}
         transposed = {}
@@ -173,33 +174,33 @@ def tile_sparselinearrelu_kernel(tc, x, weight_words, weight_scales, bias, out):
             grouped_halves[i, h] = grouped
 
         def quantise_half(i, h):
-            nc.vector.quantize_mx(
-                out=x_words_of(i, h * HALF_PASSES, HALF_PASSES),
-                scales=x_scales_of(i, h * HALF_PASSES, HALF_PASSES),
-                in_=grouped_halves[i, h][:].rearrange("p g r t -> p (g r t)"),
-            )
+            for g in range(HALF_PASSES):
+                nc.vector.quantize_mx(
+                    out=x_words_of(i, h * HALF_PASSES + g),
+                    scales=x_scales[:, i, h * HALF_PASSES + g, 0:P],
+                    in_=grouped_halves[i, h][:, g, :, :].rearrange("p r t -> p (r t)"),
+                )
 
         bias_all = keep.tile([P, N], BF16, align_bytes=64)
         spread = {}
 
         def spread_bias(group, bank):
-            spread[group] = psum.tile([P, BIAS_GROUP, P], BF16, name="bank%d" % bank)
-            for c in range(BIAS_GROUP):
-                column = group * BIAS_GROUP + c
+            spread[group] = psum.tile([P, BIAS_GROUP, N_CHUNK], BF16, name="bank%d" % bank)
+            for half in range(BIAS_GROUP):
+                row = group * BIAS_GROUP + half
                 nc.tensor.matmul(
-                    out=spread[group][:, c, :],
-                    lhsT=bias_runs[:, column : column + 1].to_broadcast([P, P]),
-                    rhs=identity_bf16[:],
+                    out=spread[group][:, half, :],
+                    lhsT=identity_bf16[:, row : row + 1].to_broadcast([P, P]),
+                    rhs=bias_rows[:],
                     start=True,
                     stop=True,
                 )
 
         def copy_bias(group):
-            nc.scalar.copy(
-                out=bias_all[:].rearrange("m (q c) -> m q c", c=BIAS_RUN)[
-                    :, :, group * BIAS_GROUP : (group + 1) * BIAS_GROUP
-                ],
-                in_=spread[group][:].rearrange("m c q -> m q c"),
+            first = group * BIAS_GROUP * N_CHUNK
+            nc.vector.tensor_copy(
+                out=bias_all[:, first : first + BIAS_GROUP * N_CHUNK],
+                in_=spread[group][:].rearrange("m h n -> m (h n)"),
             )
 
         def open_block(i, j, bank, width=N_CHUNK):
@@ -210,7 +211,7 @@ def tile_sparselinearrelu_kernel(tc, x, weight_words, weight_scales, bias, out):
             nc.tensor.matmul_mx(
                 out=sums[i, j][:],
                 lhsT=x_words_of(i, g),
-                lhsT_scale=x_scales_of(i, g),
+                lhsT_scale=x_scales[:, i, g, 0:P],
                 rhs=w_words[j][g][:, first : first + width].bitcast(FP8X4),
                 rhs_scale=w_planes[g * PLANE_ROWS : P, columns],
                 start=(g == 0),
@@ -258,26 +259,24 @@ def tile_sparselinearrelu_kernel(tc, x, weight_words, weight_scales, bias, out):
             for g in range(h * HALF_PASSES, (h + 1) * HALF_PASSES):
                 multiply_pass(i, j, g)
 
-        keep_clock_up(2)
-        spread_bias(0, 6)
-        copy_bias(0)
-        spread_bias(1, 7)
-        copy_bias(1)
+        keep_clock_up(4)
         for i in head:
             sort_half(i, 0)
         for i in head:
             transpose_half(i, 0, i)
             copy_half(i, 0)
+            if i in (1, 2):
+                spread_bias(i - 1, 5 + i)
+        for i in (0, 1):
+            quantise_half(i, 0)
+        copy_bias(0)
+        quantise_half(2, 0)
+        copy_bias(1)
+        quantise_half(3, 0)
         for i in head:
             open_block(i, 0, T_BANKS + i)
-        quantise_half(0, 0)
-        quantise_half(1, 0)
-        quantise_half(2, 0)
-        quantise_half(3, 0)
-        sort_half(0, 1)
-        sort_half(1, 1)
-        sort_half(2, 1)
-        sort_half(3, 1)
+        for i in head:
+            sort_half(i, 1)
         for g in range(HALF_PASSES):
             for i in (0, 1):
                 multiply_pass(i, 0, g)

@@ -32,6 +32,8 @@ BANKS = 8
 T_BANKS = 4
 
 HEAD_TILES = 4
+TURNED_TILES = 2
+BLOCK = 32
 HALVES = 2
 HALF_K = K // HALVES
 HALF_PASSES = PASSES // HALVES
@@ -46,10 +48,11 @@ def tile_sparselinearrelu_kernel(tc, x, weight_words, weight_scales, bias, out):
     with ExitStack() as ctx:
         ctx.enter_context(tc.manual_schedule())
         keep = ctx.enter_context(tc.tile_pool(name="keep", bufs=1))
-        x_pool = ctx.enter_context(tc.tile_pool(name="x_pool", bufs=ROW_TILES))
+        x_pool = ctx.enter_context(tc.tile_pool(name="x_pool", bufs=ROW_TILES - TURNED_TILES))
         sorted_pool = ctx.enter_context(tc.tile_pool(name="sorted_pool", bufs=8))
         grouped_pool = ctx.enter_context(tc.tile_pool(name="grouped_pool", bufs=6))
-        result_pool = ctx.enter_context(tc.tile_pool(name="result_pool", bufs=16))
+        turned_pool = ctx.enter_context(tc.tile_pool(name="turned_pool", bufs=TURNED_TILES))
+        result_pool = ctx.enter_context(tc.tile_pool(name="result_pool", bufs=20))
         psum = ctx.enter_context(tc.psum_pool(name="psum", bufs=1))
 
         w_planes = keep.tile([P, N], U8, align_bytes=SLOT_BYTES)
@@ -68,7 +71,10 @@ def tile_sparselinearrelu_kernel(tc, x, weight_words, weight_scales, bias, out):
                 out=bias_rows[0:CHUNKS, :], in_=bias.rearrange("(j n) -> j n", n=N_CHUNK)
             )
 
-        x_tiles = [x_pool.tile([P, K], BF16, name="x_tile") for i in range(ROW_TILES)]
+        x_tiles = [
+            x_pool.tile([P, K], BF16, name="x_tile") for i in range(ROW_TILES - TURNED_TILES)
+        ]
+        x_blocks = keep.tile([P, PASSES, TURNED_TILES * K_PASS], BF16, align_bytes=64)
         w_words = [
             [
                 keep.tile(
@@ -83,6 +89,19 @@ def tile_sparselinearrelu_kernel(tc, x, weight_words, weight_scales, bias, out):
             nc.sync.dma_start(
                 out=x_tiles[i][:, first_k:end_k], in_=x[i * P : (i + 1) * P, first_k:end_k]
             )
+
+        def load_x_blocks(g):
+            first_row = (ROW_TILES - TURNED_TILES) * P
+            for quadrant in (0, 2, 1, 3):
+                first_k = g * K_PASS + quadrant * P
+                nc.sync.dma_start(
+                    out=x_blocks[quadrant * BLOCK : (quadrant + 1) * BLOCK, g, :].rearrange(
+                        "r (s e) -> r s e", e=P
+                    ),
+                    in_=x[first_row:ROWS, first_k : first_k + P].rearrange(
+                        "(s r) e -> r s e", r=BLOCK
+                    ),
+                )
 
         def load_w(j, g):
             pass_bytes = weight_words[g].rearrange("p n t -> p (n t)")[
@@ -119,7 +138,7 @@ def tile_sparselinearrelu_kernel(tc, x, weight_words, weight_scales, bias, out):
             load_w(1, g)
         load_x(HEAD_TILES)
         load_w(1, PASSES - 1)
-        for i in range(HEAD_TILES + 1, ROW_TILES):
+        for i in range(HEAD_TILES + 1, ROW_TILES - TURNED_TILES):
             load_x(i)
         load_scales(2 * N_CHUNK, N)
         for j in (2, 3):
@@ -180,6 +199,36 @@ def tile_sparselinearrelu_kernel(tc, x, weight_words, weight_scales, bias, out):
                     scales=x_scales[:, i, h * HALF_PASSES + g, 0:P],
                     in_=grouped_halves[i, h][:, g, :, :].rearrange("p r t -> p (r t)"),
                 )
+
+        def sort_turned(i):
+            t = i - (ROW_TILES - TURNED_TILES)
+            sorted_x = turned_pool.tile([P, PASSES, PAIRS, P], F32, align_bytes=64, name="turned_in")
+            nc.scalar.copy(
+                out=sorted_x[:],
+                in_=x_blocks[:, :, t * K_PASS : (t + 1) * K_PASS].bitcast(F32).rearrange(
+                    "p g (q u) -> p g u q", u=PAIRS
+                ),
+            )
+            sorted_halves[i] = sorted_x
+
+        def transpose_turned(i):
+            turned = turned_pool.tile([P, PASSES, PAIRS, P], F32, align_bytes=64, name="turned_out")
+            nc.vector.transpose(
+                out=turned[:].rearrange("p g u r -> p (g u r)"),
+                in_=sorted_halves[i][:].rearrange("p g u q -> p (g u q)"),
+            )
+            transposed[i] = turned
+
+        def group_turned(i):
+            grouped = turned_pool.tile(
+                [P, PASSES, P, PACK], BF16, align_bytes=64, name="turned_grouped"
+            )
+            nc.scalar.copy(
+                out=grouped[:].bitcast(F32),
+                in_=transposed[i][:].rearrange("p g u r -> p g r u"),
+            )
+            for h in range(HALVES):
+                grouped_halves[i, h] = grouped[:, h * HALF_PASSES : (h + 1) * HALF_PASSES, :, :]
 
         bias_all = keep.tile([P, N], BF16, align_bytes=64)
         spread = {}
@@ -323,38 +372,33 @@ def tile_sparselinearrelu_kernel(tc, x, weight_words, weight_scales, bias, out):
         quantise_x(4)
         multiply(4, 0, 2)
         finish(0, 1)
-        sort_x(6)
         finish(1, 1)
+        for g in range(PASSES):
+            load_x_blocks(g)
         multiply(4, 1, 3)
         quantise_x(5)
         finish(2, 1)
         finish(3, 1)
-        sort_x(7)
         multiply(5, 0, 6)
-        turn(6, (0, 1))
-        turn(7, (4, 5))
         finish(4, 0)
         finish(4, 1)
         multiply(5, 1, 7)
-        quantise_x(6)
         finish(5, 0)
-        multiply(6, 0, 0)
-        quantise_x(7)
         finish(5, 1)
-        multiply(6, 1, 1)
-        finish(6, 0)
-        multiply(7, 0, 4)
-        finish(6, 1)
-        multiply(7, 1, 5)
-        finish(7, 0)
-        finish(7, 1)
-        banks = (2, 3, 6, 7, 0, 1, 4, 5)
-        last = (ROW_TILES - 1, CHUNKS - 1)
-        turns = [(i, j) for j in (2, 3) for i in range(ROW_TILES) if (i, j) != last]
-        for n, (i, j) in enumerate(turns):
+        straight = ROW_TILES - TURNED_TILES
+        order = [(i, j) for j in (2, 3) for i in range(straight)]
+        order += [(i, j) for i in range(straight, ROW_TILES) for j in range(CHUNKS)]
+        last = order.pop()
+        steps = (sort_turned, transpose_turned, group_turned, quantise_x)
+        first_step = 5
+        banks = (0, 1, 4, 5, 2, 3, 6, 7)
+        for n, (i, j) in enumerate(order):
             multiply(i, j, banks[n % BANKS])
             finish(i, j)
+            for t in range(TURNED_TILES):
+                if 0 <= n - first_step - t < len(steps):
+                    steps[n - first_step - t](straight + t)
         for half in range(2):
             first = half * N_CHUNK // 2
-            multiply(*last, banks[(len(turns) + half) % BANKS], first, N_CHUNK // 2)
+            multiply(*last, banks[(len(order) + half) % BANKS], first, N_CHUNK // 2)
             finish(*last, first, N_CHUNK // 2)

@@ -141,9 +141,12 @@ def tile_sparselinearrelu_kernel(tc, x, weight_words, weight_scales, bias, out):
         for i in range(HEAD_TILES + 1, ROW_TILES - TURNED_TILES):
             load_x(i)
         load_scales(2 * N_CHUNK, N)
-        for j in (2, 3):
-            for g in range(PASSES):
-                load_w(j, g)
+        for g in range(PASSES):
+            load_w(2, g)
+        for g in range(PASSES):
+            load_x_blocks(g)
+        for g in range(PASSES):
+            load_w(3, g)
 
         x_codes = keep.tile(
             [P, X_CODES_PAD + ROW_TILES * PASSES * P], U32, align_bytes=SLOT_BYTES
@@ -320,12 +323,14 @@ def tile_sparselinearrelu_kernel(tc, x, weight_words, weight_scales, bias, out):
             quantise_half(i, 0)
         copy_bias(0)
         quantise_half(2, 0)
-        copy_bias(1)
         quantise_half(3, 0)
+        sort_half(0, 1)
+        sort_half(1, 1)
+        copy_bias(1)
+        sort_half(2, 1)
+        sort_half(3, 1)
         for i in head:
             open_block(i, 0, T_BANKS + i)
-        for i in head:
-            sort_half(i, 1)
         for g in range(HALF_PASSES):
             for i in (0, 1):
                 multiply_pass(i, 0, g)
@@ -373,8 +378,6 @@ def tile_sparselinearrelu_kernel(tc, x, weight_words, weight_scales, bias, out):
         multiply(4, 0, 2)
         finish(0, 1)
         finish(1, 1)
-        for g in range(PASSES):
-            load_x_blocks(g)
         multiply(4, 1, 3)
         quantise_x(5)
         finish(2, 1)
@@ -390,7 +393,7 @@ def tile_sparselinearrelu_kernel(tc, x, weight_words, weight_scales, bias, out):
         order += [(i, j) for i in range(straight, ROW_TILES) for j in range(CHUNKS)]
         last = order.pop()
         steps = (sort_turned, transpose_turned, group_turned, quantise_x)
-        first_step = 5
+        first_step = 2
         banks = (0, 1, 4, 5, 2, 3, 6, 7)
         for n, (i, j) in enumerate(order):
             multiply(i, j, banks[n % BANKS])

from contextlib import ExitStack

import concourse.mybir as mybir
from concourse.masks import make_identity

F32 = mybir.dt.float32
BF16 = mybir.dt.bfloat16
I32 = mybir.dt.int32
U32 = mybir.dt.uint32
U8 = mybir.dt.uint8
FP8X4 = mybir.dt.float8_e4m3fn_x4

P = 128
PACK = 4
K_PASS = P * PACK
PAIRS = PACK // 2

ROWS = 1024
K = 2048
N = 2048
N_CHUNK = 512

ROW_TILES = ROWS // P
PASSES = K // K_PASS
CHUNKS = N // N_CHUNK
PLANE_ROWS = 4
QUADRANTS = 4
SLOT_BYTES = 256
X_CODES_PAD = 48

BANKS = 8
T_BANKS = 4

HEAD_TILES = 4
TURNED_TILES = 2
BLOCK = 32
HALVES = 2
HALF_K = K // HALVES
HALF_PASSES = PASSES // HALVES
BIAS_BANKS = 2
BIAS_GROUP = CHUNKS // BIAS_BANKS

FLOPS = 2 * ROWS * K * N


def tile_sparselinearrelu_kernel(tc, x, weight_words, weight_scales, bias, out):
    nc = tc.nc
    with ExitStack() as ctx:
        ctx.enter_context(tc.manual_schedule())
        keep = ctx.enter_context(tc.tile_pool(name="keep", bufs=1))
        x_pool = ctx.enter_context(tc.tile_pool(name="x_pool", bufs=ROW_TILES - TURNED_TILES))
        sorted_pool = ctx.enter_context(tc.tile_pool(name="sorted_pool", bufs=8))
        grouped_pool = ctx.enter_context(tc.tile_pool(name="grouped_pool", bufs=6))
        turned_pool = ctx.enter_context(tc.tile_pool(name="turned_pool", bufs=TURNED_TILES))
        result_pool = ctx.enter_context(tc.tile_pool(name="result_pool", bufs=20))
        psum = ctx.enter_context(tc.psum_pool(name="psum", bufs=1))

        w_planes = keep.tile([P, N], U8, align_bytes=SLOT_BYTES)
        nc.vector.memset(w_planes[:].bitcast(I32), 0)
        zeros = keep.tile([P, N_CHUNK], BF16)
        nc.vector.memset(zeros[:].bitcast(I32), 0)
        bias_rows = keep.tile([P, N_CHUNK], BF16)
        nc.gpsimd.memset(bias_rows[:], 0.0)
        identity = keep.tile([P, P], F32)
        make_identity(nc, identity[:])
        identity_bf16 = keep.tile([P, P], BF16)
        nc.scalar.copy(out=identity_bf16[:], in_=identity[:])

        def load_bias():
            nc.sync.dma_start(
                out=bias_rows[0:CHUNKS, :], in_=bias.rearrange("(j n) -> j n", n=N_CHUNK)
            )

        x_tiles = [
            x_pool.tile([P, K], BF16, name="x_tile") for i in range(ROW_TILES - TURNED_TILES)
        ]
        x_blocks = keep.tile([P, PASSES, TURNED_TILES * K_PASS], BF16, align_bytes=64)
        w_words = [
            [
                keep.tile(
                    [P, N_CHUNK], U32, name="w_words_%d_%d" % (j, g), align_bytes=SLOT_BYTES
                )
                for g in range(PASSES)
            ]
            for j in range(CHUNKS)
        ]

        def load_x(i, first_k=0, end_k=K):
            nc.sync.dma_start(
                out=x_tiles[i][:, first_k:end_k], in_=x[i * P : (i + 1) * P, first_k:end_k]
            )

        def load_x_blocks(g):
            first_row = (ROW_TILES - TURNED_TILES) * P
            for quadrant in (0, 2, 1, 3):
                first_k = g * K_PASS + quadrant * P
                nc.sync.dma_start(
                    out=x_blocks[quadrant * BLOCK : (quadrant + 1) * BLOCK, g, :].rearrange(
                        "r (s e) -> r s e", e=P
                    ),
                    in_=x[first_row:ROWS, first_k : first_k + P].rearrange(
                        "(s r) e -> r s e", r=BLOCK
                    ),
                )

        def load_w(j, g):
            pass_bytes = weight_words[g].rearrange("p n t -> p (n t)")[
                :, j * N_CHUNK * PACK : (j + 1) * N_CHUNK * PACK
            ]
            nc.sync.dma_start(out=w_words[j][g][:].bitcast(I32), in_=pass_bytes.bitcast(I32))

        def load_scales(first_column, end_column):
            for quadrant in range(QUADRANTS):
                first_partition = quadrant * (P // QUADRANTS)
                nc.sync.dma_start(
                    out=w_planes[
                        first_partition : first_partition + PASSES * PLANE_ROWS,
                        first_column:end_column,
                    ].bitcast(I32),
                    in_=weight_scales[
                        :,
                        quadrant * PLANE_ROWS : (quadrant + 1) * PLANE_ROWS,
                        first_column:end_column,
                    ].bitcast(I32),
                )

        for h in range(HALVES):
            for i in range(HEAD_TILES):
                load_x(i, h * HALF_K, (h + 1) * HALF_K)
                if (i, h) == (1, 0):
                    load_bias()
            if h == 0:
                load_scales(0, N_CHUNK)
            for g in range(h * HALF_PASSES, (h + 1) * HALF_PASSES):
                load_w(0, g)
        load_scales(N_CHUNK, 2 * N_CHUNK)
        for g in range(PASSES - 1):
            load_w(1, g)
        load_x(HEAD_TILES)
        load_w(1, PASSES - 1)
        for i in range(HEAD_TILES + 1, ROW_TILES - TURNED_TILES):
            load_x(i)
        load_scales(2 * N_CHUNK, N)
        for g in range(PASSES):
            load_w(2, g)
        for g in range(PASSES):
            load_x_blocks(g)
        for g in range(PASSES):
            load_w(3, g)

        x_codes = keep.tile(
            [P, X_CODES_PAD + ROW_TILES * PASSES * P], U32, align_bytes=SLOT_BYTES
        )
        x_scales = keep.tile([P, ROW_TILES, PASSES, SLOT_BYTES], U8, align_bytes=SLOT_BYTES)

        def x_words_of(i, g):
            first_code_word = X_CODES_PAD + (i * PASSES + g) * P
            return x_codes[:, first_code_word : first_code_word + P].bitcast(FP8X4)

        sorted_halves = {}
        transposed = {}
        grouped_halves = {}
        sums = {}
        results = {}

        def sort_half(i, h):
            sorted_x = sorted_pool.tile([P, HALF_PASSES, PAIRS, P], F32, name="sorted_x")
            nc.vector.tensor_copy(
                out=sorted_x[:],
                in_=x_tiles[i][:, h * HALF_K : (h + 1) * HALF_K].bitcast(F32).rearrange(
                    "r (g p u) -> r g u p", g=HALF_PASSES, u=PAIRS
                ),
            )
            sorted_halves[i, h] = sorted_x

        def transpose_half(i, h, bank):
            xt = psum.tile([P, HALF_PASSES, PAIRS, P], F32, name="bank%d" % bank)
            words = x_tiles[i][:, h * HALF_K : (h + 1) * HALF_K].bitcast(F32)
            for g in range(HALF_PASSES):
                for u in range(PAIRS):
                    if (i, h) in sorted_halves:
                        source = sorted_halves[i, h][:, g, u, :]
                    else:
                        source = words[:, PAIRS * P * g + u : PAIRS * P * (g + 1) : PAIRS]
                    nc.tensor.transpose(xt[:, g, u, :], source, identity[:])
            transposed[i, h] = xt

        def copy_half(i, h, copy=nc.scalar.copy):
            grouped = grouped_pool.tile(
                [P, HALF_PASSES, P, PACK], BF16, align_bytes=64, name="grouped"
            )
            copy(
                out=grouped[:].bitcast(F32),
                in_=transposed[i, h][:].rearrange("p g u r -> p g r u"),
            )
            grouped_halves[i, h] = grouped

        def quantise_half(i, h):
            for g in range(HALF_PASSES):
                nc.vector.quantize_mx(
                    out=x_words_of(i, h * HALF_PASSES + g),
                    scales=x_scales[:, i, h * HALF_PASSES + g, 0:P],
                    in_=grouped_halves[i, h][:, g, :, :].rearrange("p r t -> p (r t)"),
                )

        def sort_turned(i):
            t = i - (ROW_TILES - TURNED_TILES)
            sorted_x = turned_pool.tile([P, PASSES, PAIRS, P], F32, align_bytes=64, name="turned_in")
            nc.scalar.copy(
                out=sorted_x[:],
                in_=x_blocks[:, :, t * K_PASS : (t + 1) * K_PASS].bitcast(F32).rearrange(
                    "p g (q u) -> p g u q", u=PAIRS
                ),
            )
            sorted_halves[i] = sorted_x

        def transpose_turned(i):
            turned = turned_pool.tile([P, PASSES, PAIRS, P], F32, align_bytes=64, name="turned_out")
            nc.vector.transpose(
                out=turned[:].rearrange("p g u r -> p (g u r)"),
                in_=sorted_halves[i][:].rearrange("p g u q -> p (g u q)"),
            )
            transposed[i] = turned

        def group_turned(i):
            grouped = turned_pool.tile(
                [P, PASSES, P, PACK], BF16, align_bytes=64, name="turned_grouped"
            )
            nc.scalar.copy(
                out=grouped[:].bitcast(F32),
                in_=transposed[i][:].rearrange("p g u r -> p g r u"),
            )
            for h in range(HALVES):
                grouped_halves[i, h] = grouped[:, h * HALF_PASSES : (h + 1) * HALF_PASSES, :, :]

        bias_all = keep.tile([P, N], BF16, align_bytes=64)
        spread = {}

        def spread_bias(group, bank):
            spread[group] = psum.tile([P, BIAS_GROUP, N_CHUNK], BF16, name="bank%d" % bank)
            for half in range(BIAS_GROUP):
                row = group * BIAS_GROUP + half
                nc.tensor.matmul(
                    out=spread[group][:, half, :],
                    lhsT=identity_bf16[:, row : row + 1].to_broadcast([P, P]),
                    rhs=bias_rows[:],
                    start=True,
                    stop=True,
                )

        def copy_bias(group):
            first = group * BIAS_GROUP * N_CHUNK
            nc.vector.tensor_copy(
                out=bias_all[:, first : first + BIAS_GROUP * N_CHUNK],
                in_=spread[group][:].rearrange("m h n -> m (h n)"),
            )

        def open_block(i, j, bank, width=N_CHUNK):
            sums[i, j] = psum.tile([P, width], F32, name="bank%d" % bank)

        def multiply_pass(i, j, g, first=0, width=N_CHUNK):
            columns = slice(j * N_CHUNK + first, j * N_CHUNK + first + width)
            nc.tensor.matmul_mx(
                out=sums[i, j][:],
                lhsT=x_words_of(i, g),
                lhsT_scale=x_scales[:, i, g, 0:P],
                rhs=w_words[j][g][:, first : first + width].bitcast(FP8X4),
                rhs_scale=w_planes[g * PLANE_ROWS : P, columns],
                start=(g == 0),
                stop=(g == PASSES - 1),
            )

        def multiply(i, j, bank, first=0, width=N_CHUNK):
            open_block(i, j, bank, width)
            for g in range(PASSES):
                multiply_pass(i, j, g, first, width)

        def add_bias(i, j, first=0, width=N_CHUNK):
            columns = slice(j * N_CHUNK + first, j * N_CHUNK + first + width)
            results[i, j] = result_pool.tile([P, width], F32, name="result")
            nc.vector.tensor_tensor(
                out=results[i, j][:], in0=sums[i, j][:], in1=bias_all[:, columns],
                op=mybir.AluOpType.add,
            )

        def relu_and_store(i, j, first=0, width=N_CHUNK):
            columns = slice(j * N_CHUNK + first, j * N_CHUNK + first + width)
            nc.scalar.activation(
                out=results[i, j][:], in_=results[i, j][:],
                func=mybir.ActivationFunctionType.Relu,
            )
            nc.sync.dma_start(out=out[i * P : (i + 1) * P, columns], in_=results[i, j][:])

        def finish(i, j, first=0, width=N_CHUNK):
            add_bias(i, j, first, width)
            relu_and_store(i, j, first, width)

        def keep_clock_up_in(bank, count):
            unread = psum.tile([P, N_CHUNK], F32, name="bank%d" % bank)
            for repeat in range(count):
                nc.tensor.matmul(
                    out=unread[:], lhsT=zeros[:, 0:P], rhs=zeros[:], start=True, stop=True
                )

        def keep_clock_up(count):
            keep_clock_up_in(4, count)

        head = range(HEAD_TILES)

        def multiply_half(i, j, h):
            for g in range(h * HALF_PASSES, (h + 1) * HALF_PASSES):
                multiply_pass(i, j, g)

        keep_clock_up(4)
        for i in head:
            sort_half(i, 0)
        for i in head:
            transpose_half(i, 0, i)
            copy_half(i, 0)
            if i in (1, 2):
                spread_bias(i - 1, 5 + i)
        for i in (0, 1):
            quantise_half(i, 0)
        copy_bias(0)
        quantise_half(2, 0)
        quantise_half(3, 0)
        sort_half(0, 1)
        sort_half(1, 1)
        copy_bias(1)
        sort_half(2, 1)
        sort_half(3, 1)
        for i in head:
            open_block(i, 0, T_BANKS + i)
        for g in range(HALF_PASSES):
            for i in (0, 1):
                multiply_pass(i, 0, g)
        multiply_half(2, 0, 0)
        transpose_half(0, 1, 0)
        transpose_half(1, 1, 1)
        multiply_half(3, 0, 0)
        transpose_half(2, 1, 2)
        transpose_half(3, 1, 3)
        for i in head:
            copy_half(i, 1)
            quantise_half(i, 1)
        for i in head:
            multiply_half(i, 0, 1)

        for i in head:
            finish(i, 0)
            open_block(i, 1, (0, 1, 4, 5)[i])
        for i in head:
            multiply_half(i, 1, 0)
        for i in head:
            multiply_pass(i, 1, 2)

        def turn(i, banks):
            for h in range(HALVES):
                transpose_half(i, h, banks[h])
            for h in range(HALVES):
                copy_half(i, h)

        def sort_x(i):
            for h in range(HALVES):
                sort_half(i, h)

        def quantise_x(i):
            for h in range(HALVES):
                quantise_half(i, h)

        sort_x(4)
        sort_x(5)
        turn(4, (2, 3))
        turn(5, (6, 7))
        for i in head:
            multiply_pass(i, 1, PASSES - 1)
        quantise_x(4)
        multiply(4, 0, 2)
        finish(0, 1)
        finish(1, 1)
        multiply(4, 1, 3)
        quantise_x(5)
        finish(2, 1)
        finish(3, 1)
        multiply(5, 0, 6)
        finish(4, 0)
        finish(4, 1)
        multiply(5, 1, 7)
        finish(5, 0)
        finish(5, 1)
        straight = ROW_TILES - TURNED_TILES
        order = [(i, j) for j in (2, 3) for i in range(straight)]
        order += [(i, j) for i in range(straight, ROW_TILES) for j in range(CHUNKS)]
        last = order.pop()
        steps = (sort_turned, transpose_turned, group_turned, quantise_x)
        first_step = 2
        banks = (0, 1, 4, 5, 2, 3, 6, 7)
        for n, (i, j) in enumerate(order):
            multiply(i, j, banks[n % BANKS])
            finish(i, j)
            for t in range(TURNED_TILES):
                if 0 <= n - first_step - t < len(steps):
                    steps[n - first_step - t](straight + t)
        for half in range(2):
            first = half * N_CHUNK // 2
            multiply(*last, banks[(len(order) + half) % BANKS], first, N_CHUNK // 2)
            finish(*last, first, N_CHUNK // 2)
